import numpy as np
import ml_dtypes


def mxq(x, axis, fmt="e4m3"):
    dtype, down = {"e4m3": (ml_dtypes.float8_e4m3fn, 7), "e5m2": (ml_dtypes.float8_e5m2, 14)}[fmt]
    v = np.moveaxis(np.asarray(x, np.float32).astype(ml_dtypes.bfloat16).astype(np.float64), axis, -1)
    blocks = v.reshape(v.shape[:-1] + (-1, 32))
    amax = np.abs(blocks).max(-1, keepdims=True)
    byte = np.maximum(np.where(amax > 0, np.frexp(amax)[1] - 1 + 127, 0) - down, 1)
    scale = np.exp2(byte - 127.0)
    codes = (blocks / scale).astype(np.float32).astype(dtype).astype(np.float64)
    return np.moveaxis((codes * scale).reshape(v.shape), -1, axis)


WIDE = False


def mx_kscale(k):
    if not WIDE:
        return np.ones(k)
    levels = np.array([10, -10, 5, -5, 0])
    a = np.random.permutation(np.resize(levels, k // 512 * 4)).reshape(k // 512, 4)
    idx = np.arange(k)
    return np.exp2(a[idx // 512, idx % 128 // 32])


BF16 = ml_dtypes.bfloat16


def bf(x):
    return np.asarray(x, np.float32).astype(BF16)


def f64(x):
    return np.asarray(x).astype(np.float64)


B, S, DV, DL, D = 8, 512, 1024, 1024, 512
EPS = 1e-5
SIGMA = 1.7


def layernorm(x, g, b):
    m = x.mean(-1, keepdims=True)
    v = np.square(x - m).mean(-1, keepdims=True)
    return (x - m) / np.sqrt(v + EPS) * g + b


def setup_inputs():
    t = mx_kscale(D + D)
    z = SIGMA * np.random.standard_normal((B, S, S))
    e = np.exp(z - z.max(-1, keepdims=True))
    return {
        'A': bf(e / e.sum(-1, keepdims=True)),
        'vp': bf(np.maximum(np.random.standard_normal((B, S, D)), 0.0) * t[:D]),
        'lp': bf(np.maximum(np.random.standard_normal((B, S, D)), 0.0) * t[D:]),
        'oW': bf(np.random.standard_normal((D + D, D)) / np.sqrt(D + D) / t[:, None]),
        'ob': bf(0.1 * np.random.standard_normal(D)),
        'og': bf(1.0 + 0.1 * np.random.standard_normal(D)),
        'obeta': bf(0.1 * np.random.standard_normal(D)),
    }


def reference(A, vp, lp, oW, ob, og, obeta):
    a = f64(A)
    aligned_vision = mxq(a, 2, 'e4m3') @ mxq(f64(vp), 1, 'e4m3')
    aligned_language = mxq(a, 1, 'e4m3').transpose(0, 2, 1) @ mxq(f64(lp), 1, 'e4m3')
    combined = np.concatenate([aligned_vision, aligned_language], axis=-1)
    h = (mxq(combined, 2, 'e4m3') @ mxq(f64(oW), 0, 'e4m3')) + f64(ob)
    return np.maximum(layernorm(h, f64(og), f64(obeta)), 0.0)

@@ -1,0 +1,222 @@
+from contextlib import ExitStack
+
+import concourse.mybir as mybir
+from concourse.masks import make_identity
+
+F32 = mybir.dt.float32
+BF16 = mybir.dt.bfloat16
+U32 = mybir.dt.uint32
+U8 = mybir.dt.uint8
+FP8X4 = mybir.dt.float8_e4m3fn_x4
+ALU = mybir.AluOpType
+ACT = mybir.ActivationFunctionType
+
+B = 8
+S = 512
+D = 512
+P = 128
+PACK = 4
+NT = S // P
+EPS = 1e-5
+
+FLOPS = 2 * B * S * S * D * 2 + 2 * B * S * (2 * D) * D
+
+
+def regroup(copy, dst, src):
+    copy(
+        out=dst.rearrange("p (c i) t -> p c t i", i=4),
+        in_=src.rearrange("p t (c i) -> p c t i", i=4),
+    )
+
+
+def tile_clawmatrix_pb_t_kernel(tc, A, vp, lp, oW, ob, og, obeta, out):
+    nc = tc.nc
+    with ExitStack() as ctx:
+        const = ctx.enter_context(tc.tile_pool(name="const", bufs=1))
+        raw = ctx.enter_context(tc.tile_pool(name="raw", bufs=3))
+        grp = ctx.enter_context(tc.tile_pool(name="grp", bufs=2))
+        code = ctx.enter_context(tc.tile_pool(name="code", bufs=2))
+        comb = ctx.enter_context(tc.tile_pool(name="comb", bufs=2))
+        epi = ctx.enter_context(tc.tile_pool(name="epi", bufs=3))
+        small = ctx.enter_context(tc.tile_pool(name="small", bufs=3))
+        ps_t = ctx.enter_context(tc.psum_pool(name="ps_t", bufs=2))
+        ps_c = ctx.enter_context(tc.psum_pool(name="ps_c", bufs=4))
+        ps_h = ctx.enter_context(tc.psum_pool(name="ps_h", bufs=2))
+
+        eps_t = const.tile([P, 1], F32)
+        nc.vector.memset(eps_t[:], EPS)
+        warm = const.tile([P, 1], F32)
+        nc.scalar.activation(out=warm[:], in_=eps_t[:], func=ACT.Sqrt)
+        ident = const.tile([P, P], F32)
+        make_identity(nc, ident[:])
+        ones = const.tile([P, P], BF16)
+        nc.vector.memset(ones[:], 1.0)
+        vecs = const.tile([P, 3, D], BF16)
+        nc.vector.memset(vecs[:], 0.0)
+
+        state = {}
+
+        def load(b):
+            rawA = raw.tile([P, NT, S], BF16, name="rawA")
+            nc.sync.dma_start(out=rawA[:], in_=A[b].rearrange("(i p) t -> p i t", p=P))
+            rawV = raw.tile([P, PACK, D], BF16, name="rawV")
+            nc.sync.dma_start(
+                out=rawV[:].rearrange("p (u e) d -> p u (e d)", e=2),
+                in_=vp[b].rearrange("(u p e) d -> p u (e d)", u=2, e=2),
+            )
+            rawL = raw.tile([P, NT, D], BF16, name="rawL")
+            nc.sync.dma_start(out=rawL[:], in_=lp[b].rearrange("(i p) d -> p i d", p=P))
+            state[("raw", b)] = (rawA, rawV, rawL)
+
+        def prep(b):
+            rawA, rawV, rawL = state[("raw", b)]
+            gAT = grp.tile([P, S * PACK], BF16, name="gAT", align_bytes=64)
+            gAT32 = gAT[:].bitcast(F32).rearrange("p (s u) -> p s u", u=2)
+            for h in range(2):
+                xt = ps_t.tile([P, 2, 2 * P], F32, name="xt")
+                for ii in range(2):
+                    words = rawA[:, 2 * h + ii, :].bitcast(F32)
+                    for u in range(2):
+                        nc.tensor.transpose(
+                            xt[:, u, P * ii : P * ii + P],
+                            words[:, P * u : P * u + P],
+                            ident[:],
+                        )
+                nc.scalar.copy(
+                    out=gAT32[:, 2 * P * h : 2 * P * h + 2 * P, :],
+                    in_=xt[:].rearrange("p u s -> p s u"),
+                )
+            gV = grp.tile([P, D, PACK], BF16, name="gV", align_bytes=64)
+            regroup(nc.scalar.copy, gV[:], rawV[:])
+            gA = grp.tile([P, S, PACK], BF16, name="gA", align_bytes=64)
+            regroup(nc.vector.tensor_copy, gA[:], rawA[:])
+            gL = grp.tile([P, D, PACK], BF16, name="gL", align_bytes=64)
+            regroup(nc.vector.tensor_copy, gL[:], rawL[:])
+            res = []
+            for nm, g2 in (
+                ("A", gA[:].rearrange("p w t -> p (w t)")),
+                ("L", gL[:].rearrange("p w t -> p (w t)")),
+                ("T", gAT[:]),
+                ("V", gV[:].rearrange("p w t -> p (w t)")),
+            ):
+                cw = code.tile([P, S], U32, name="cw" + nm, align_bytes=64)
+                sc = code.tile([P, S], U8, name="sc" + nm, align_bytes=64)
+                nc.vector.quantize_mx(out=cw[:].bitcast(FP8X4), scales=sc[:], in_=g2)
+                res.append((cw, sc))
+            state[("q", b)] = res
+
+        def stage1(b):
+            (cA, sA), (cL, sL), (cT, sT), (cV, sV) = state[("q", b)]
+            cg = comb.tile([P, 2, S, PACK], BF16, name="cg", align_bytes=64)
+            cc = comb.tile([P, 2, S], U32, name="cc", align_bytes=64)
+            cs = comb.tile([P, 2, S], U8, name="cs", align_bytes=64)
+            for g, (xc, xs, yc, ys) in enumerate(((cV, sV, cT, sT), (cL, sL, cA, sA))):
+                for k in range(NT):
+                    cp = ps_c.tile([P, PACK, P], F32, name="cp")
+                    cols = slice(P * k, P * k + P)
+                    for t in range(PACK):
+                        mcols = slice(P * t, P * t + P)
+                        nc.tensor.matmul_mx(
+                            out=cp[:, t, :],
+                            lhsT=xc[:, mcols].bitcast(FP8X4),
+                            lhsT_scale=xs[:, mcols],
+                            rhs=yc[:, cols].bitcast(FP8X4),
+                            rhs_scale=ys[:, cols],
+                            start=True,
+                            stop=True,
+                        )
+                    nc.scalar.copy(out=cg[:, g, cols, :], in_=cp[:].rearrange("p t s -> p s t"))
+                nc.vector.quantize_mx(
+                    out=cc[:, g, :].bitcast(FP8X4),
+                    scales=cs[:, g, :],
+                    in_=cg[:, g].rearrange("p s t -> p (s t)"),
+                )
+            state[("c", b)] = (cc, cs)
+
+        def stage2(b):
+            cc, cs = state[("c", b)]
+            w = epi.tile([P, NT, D], F32, name="w", bufs=2)
+            y = epi.tile([P, NT, D], F32, name="y")
+            sums = small.tile([P, NT], F32, name="sums")
+            negmean = small.tile([P, NT], F32, name="negmean")
+            ssq = small.tile([P, NT], F32, name="ssq")
+            std = small.tile([P, NT], F32, name="std")
+            rstd = small.tile([P, NT], F32, name="rstd")
+            for i in range(NT):
+                hp = ps_h.tile([P, D], F32, name="hp")
+                cols = slice(P * i, P * i + P)
+                for g in range(2):
+                    nc.tensor.matmul_mx(
+                        out=hp[:],
+                        lhsT=cc[:, g, cols].bitcast(FP8X4),
+                        lhsT_scale=cs[:, g, cols],
+                        rhs=Wc[:, g, :].bitcast(FP8X4),
+                        rhs_scale=Ws[:, g, :],
+                        start=(g == 0),
+                        stop=(g == 1),
+                    )
+                nc.vector.scalar_tensor_tensor(
+                    out=w[:, i, :], in0=hp[:], scalar=1.0, in1=ob_b[:],
+                    op0=ALU.mult, op1=ALU.add, accum_out=sums[:, i : i + 1],
+                )
+            nc.vector.tensor_scalar(
+                out=negmean[:], in0=sums[:], scalar1=-1.0 / D, scalar2=None, op0=ALU.mult
+            )
+            for i in range(NT):
+                junk = epi.tile([P, D], BF16, name="junk")
+                nc.scalar.activation(
+                    out=junk[:], in_=w[:, i, :], func=ACT.Square,
+                    bias=negmean[:, i : i + 1], scale=1.0, accum_out=ssq[:, i : i + 1],
+                )
+            for i in range(NT):
+                nc.vector.scalar_tensor_tensor(
+                    out=y[:, i, :], in0=w[:, i, :], scalar=negmean[:, i : i + 1], in1=g_b[:],
+                    op0=ALU.add, op1=ALU.mult,
+                )
+            nc.scalar.activation(out=std[:], in_=ssq[:], func=ACT.Sqrt, bias=eps_t[:], scale=1.0 / D)
+            nc.vector.reciprocal(out=rstd[:], in_=std[:])
+            dst = out[b].rearrange("(i p) e -> p i e", p=P)
+            for i in range(NT):
+                nc.vector.scalar_tensor_tensor(
+                    out=y[:, i, :], in0=y[:, i, :], scalar=rstd[:, i : i + 1], in1=beta_b[:],
+                    op0=ALU.mult, op1=ALU.add,
+                )
+                nc.scalar.activation(out=y[:, i, :], in_=y[:, i, :], func=ACT.Relu)
+                nc.sync.dma_start(out=dst[:, i, :], in_=y[:, i, :])
+
+        load(0)
+        for v, vec in enumerate((ob, og, obeta)):
+            nc.sync.dma_start(out=vecs[0:1, v, :], in_=vec.unsqueeze(0))
+        rawW = const.tile([P, 2 * PACK, D], BF16)
+        nc.sync.dma_start(out=rawW[:], in_=oW.rearrange("(j p) n -> p j n", p=P))
+        load(1)
+        prep(0)
+
+        bc = []
+        for v in range(3):
+            bp = ps_h.tile([P, D], F32, name="hp")
+            nc.tensor.matmul(out=bp[:], lhsT=ones[:], rhs=vecs[:, v, :], start=True, stop=True)
+            bt = const.tile([P, D], F32, name="bc%d" % v)
+            nc.vector.tensor_copy(out=bt[:], in_=bp[:])
+            bc.append(bt)
+        ob_b, g_b, beta_b = bc
+
+        gW = const.tile([P, 2, D, PACK], BF16, align_bytes=64)
+        Wc = const.tile([P, 2, D], U32, align_bytes=64)
+        Ws = const.tile([P, 2, D], U8, align_bytes=64)
+        for g in range(2):
+            regroup(nc.vector.tensor_copy, gW[:, g], rawW[:, PACK * g : PACK * g + PACK, :])
+        for g in range(2):
+            nc.vector.quantize_mx(
+                out=Wc[:, g, :].bitcast(FP8X4),
+                scales=Ws[:, g, :],
+                in_=gW[:, g].rearrange("p n t -> p (n t)"),
+            )
+
+        for b in range(B):
+            if b + 2 < B:
+                load(b + 2)
+            stage1(b)
+            if b + 1 < B:
+                prep(b + 1)
+            stage2(b)

@@ -18,6 +18,8 @@ P = 128
 PACK = 4
 NT = S // P
 EPS = 1e-5
+LV = 128
+BIG = 3.0e38
 
 FLOPS = 2 * B * S * S * D * 2 + 2 * B * S * (2 * D) * D
 
@@ -40,7 +42,8 @@ def tile_clawmatrix_pb_t_kernel(tc, A, vp, lp, oW, ob, og, obeta, out):
         epi = ctx.enter_context(tc.tile_pool(name="epi", bufs=3))
         small = ctx.enter_context(tc.tile_pool(name="small", bufs=3))
         ps_t = ctx.enter_context(tc.psum_pool(name="ps_t", bufs=2))
-        ps_c = ctx.enter_context(tc.psum_pool(name="ps_c", bufs=4))
+        ps_c = ctx.enter_context(tc.psum_pool(name="ps_c", bufs=2))
+        ps_k = ctx.enter_context(tc.psum_pool(name="ps_k", bufs=1))
         ps_h = ctx.enter_context(tc.psum_pool(name="ps_h", bufs=2))
 
         eps_t = const.tile([P, 1], F32)
@@ -91,7 +94,8 @@ def tile_clawmatrix_pb_t_kernel(tc, A, vp, lp, oW, ob, og, obeta, out):
             gA = grp.tile([P, S, PACK], BF16, name="gA", align_bytes=64)
             regroup(nc.vector.tensor_copy, gA[:], rawA[:])
             gL = grp.tile([P, D, PACK], BF16, name="gL", align_bytes=64)
-            regroup(nc.vector.tensor_copy, gL[:], rawL[:])
+            regroup(nc.vector.tensor_copy, gL[:, 0:LV, :], rawL[:, :, 0:LV])
+            regroup(nc.scalar.copy, gL[:, LV:D, :], rawL[:, :, LV:D])
             res = []
             for nm, g2 in (
                 ("A", gA[:].rearrange("p w t -> p (w t)")),
@@ -181,7 +185,9 @@ def tile_clawmatrix_pb_t_kernel(tc, A, vp, lp, oW, ob, og, obeta, out):
                     out=y[:, i, :], in0=y[:, i, :], scalar=rstd[:, i : i + 1], in1=beta_b[:],
                     op0=ALU.mult, op1=ALU.add,
                 )
-                nc.scalar.activation(out=y[:, i, :], in_=y[:, i, :], func=ACT.Relu)
+                nc.gpsimd.tensor_scalar(
+                    out=y[:, i, :], in0=y[:, i, :], scalar1=BIG, scalar2=0.0, op0=ALU.min, op1=ALU.max
+                )
                 nc.sync.dma_start(out=dst[:, i, :], in_=y[:, i, :])
 
         load(0)
@@ -192,20 +198,20 @@ def tile_clawmatrix_pb_t_kernel(tc, A, vp, lp, oW, ob, og, obeta, out):
         load(1)
         prep(0)
 
-        bc = []
-        for v in range(3):
-            bp = ps_h.tile([P, D], F32, name="hp")
-            nc.tensor.matmul(out=bp[:], lhsT=ones[:], rhs=vecs[:, v, :], start=True, stop=True)
-            bt = const.tile([P, D], F32, name="bc%d" % v)
-            nc.vector.tensor_copy(out=bt[:], in_=bp[:])
-            bc.append(bt)
-        ob_b, g_b, beta_b = bc
+        bp = ps_h.tile([P, D], F32, name="hp")
+        nc.tensor.matmul(out=bp[:], lhsT=ones[:], rhs=vecs[:, 0, :], start=True, stop=True)
+        ob_b = const.tile([P, D], F32)
+        nc.scalar.copy(out=ob_b[:], in_=bp[:])
+        g_b = ps_k.tile([P, D], F32)
+        nc.tensor.matmul(out=g_b[:], lhsT=ones[:], rhs=vecs[:, 1, :], start=True, stop=True)
+        beta_b = ps_k.tile([P, D], F32)
+        nc.tensor.matmul(out=beta_b[:], lhsT=ones[:], rhs=vecs[:, 2, :], start=True, stop=True)
 
         gW = const.tile([P, 2, D, PACK], BF16, align_bytes=64)
         Wc = const.tile([P, 2, D], U32, align_bytes=64)
         Ws = const.tile([P, 2, D], U8, align_bytes=64)
         for g in range(2):
-            regroup(nc.vector.tensor_copy, gW[:, g], rawW[:, PACK * g : PACK * g + PACK, :])
+            regroup(nc.scalar.copy, gW[:, g], rawW[:, PACK * g : PACK * g + PACK, :])
         for g in range(2):
             nc.vector.quantize_mx(
                 out=Wc[:, g, :].bitcast(FP8X4),

@@ -35,16 +35,17 @@ def tile_clawmatrix_pb_t_kernel(tc, A, vp, lp, oW, ob, og, obeta, out):
     nc = tc.nc
     with ExitStack() as ctx:
         const = ctx.enter_context(tc.tile_pool(name="const", bufs=1))
-        raw = ctx.enter_context(tc.tile_pool(name="raw", bufs=3))
+        raw = ctx.enter_context(tc.tile_pool(name="raw", bufs=4))
         grp = ctx.enter_context(tc.tile_pool(name="grp", bufs=2))
+        grp1 = ctx.enter_context(tc.tile_pool(name="grp1", bufs=1))
         code = ctx.enter_context(tc.tile_pool(name="code", bufs=2))
         comb = ctx.enter_context(tc.tile_pool(name="comb", bufs=2))
         epi = ctx.enter_context(tc.tile_pool(name="epi", bufs=3))
         small = ctx.enter_context(tc.tile_pool(name="small", bufs=3))
-        ps_t = ctx.enter_context(tc.psum_pool(name="ps_t", bufs=2))
+        ps_t = ctx.enter_context(tc.psum_pool(name="ps_t", bufs=1))
         ps_c = ctx.enter_context(tc.psum_pool(name="ps_c", bufs=2))
         ps_k = ctx.enter_context(tc.psum_pool(name="ps_k", bufs=1))
-        ps_h = ctx.enter_context(tc.psum_pool(name="ps_h", bufs=2))
+        ps_h = ctx.enter_context(tc.psum_pool(name="ps_h", bufs=3))
 
         eps_t = const.tile([P, 1], F32)
         nc.vector.memset(eps_t[:], EPS)
@@ -57,9 +58,11 @@ def tile_clawmatrix_pb_t_kernel(tc, A, vp, lp, oW, ob, og, obeta, out):
         vecs = const.tile([P, 3, D], BF16)
         nc.vector.memset(vecs[:], 0.0)
 
-        state = {}
+        raws, grps, codes, combs, lns = {}, {}, {}, {}, {}
 
         def load(b):
+            if not 0 <= b < B:
+                return
             rawA = raw.tile([P, NT, S], BF16, name="rawA")
             nc.sync.dma_start(out=rawA[:], in_=A[b].rearrange("(i p) t -> p i t", p=P))
             rawV = raw.tile([P, PACK, D], BF16, name="rawV")
@@ -69,160 +72,309 @@ def tile_clawmatrix_pb_t_kernel(tc, A, vp, lp, oW, ob, og, obeta, out):
             )
             rawL = raw.tile([P, NT, D], BF16, name="rawL")
             nc.sync.dma_start(out=rawL[:], in_=lp[b].rearrange("(i p) d -> p i d", p=P))
-            state[("raw", b)] = (rawA, rawV, rawL)
+            raws[b] = {"A": rawA, "V": rawV, "L": rawL}
 
-        def prep(b):
-            rawA, rawV, rawL = state[("raw", b)]
-            gAT = grp.tile([P, S * PACK], BF16, name="gAT", align_bytes=64)
-            gAT32 = gAT[:].bitcast(F32).rearrange("p (s u) -> p s u", u=2)
-            for h in range(2):
-                xt = ps_t.tile([P, 2, 2 * P], F32, name="xt")
-                for ii in range(2):
-                    words = rawA[:, 2 * h + ii, :].bitcast(F32)
-                    for u in range(2):
-                        nc.tensor.transpose(
-                            xt[:, u, P * ii : P * ii + P],
-                            words[:, P * u : P * u + P],
-                            ident[:],
-                        )
-                nc.scalar.copy(
-                    out=gAT32[:, 2 * P * h : 2 * P * h + 2 * P, :],
-                    in_=xt[:].rearrange("p u s -> p s u"),
-                )
-            gV = grp.tile([P, D, PACK], BF16, name="gV", align_bytes=64)
-            regroup(nc.scalar.copy, gV[:], rawV[:])
-            gA = grp.tile([P, S, PACK], BF16, name="gA", align_bytes=64)
-            regroup(nc.vector.tensor_copy, gA[:], rawA[:])
-            gL = grp.tile([P, D, PACK], BF16, name="gL", align_bytes=64)
-            regroup(nc.vector.tensor_copy, gL[:, 0:LV, :], rawL[:, :, 0:LV])
-            regroup(nc.scalar.copy, gL[:, LV:D, :], rawL[:, :, LV:D])
-            res = []
-            for nm, g2 in (
-                ("A", gA[:].rearrange("p w t -> p (w t)")),
-                ("L", gL[:].rearrange("p w t -> p (w t)")),
-                ("T", gAT[:]),
-                ("V", gV[:].rearrange("p w t -> p (w t)")),
-            ):
-                cw = code.tile([P, S], U32, name="cw" + nm, align_bytes=64)
-                sc = code.tile([P, S], U8, name="sc" + nm, align_bytes=64)
-                nc.vector.quantize_mx(out=cw[:].bitcast(FP8X4), scales=sc[:], in_=g2)
-                res.append((cw, sc))
-            state[("q", b)] = res
+        def grouped(b, nm):
+            if (b, nm) not in grps:
+                pool = grp1 if nm == "A" else grp
+                grps[b, nm] = pool.tile([P, S, PACK], BF16, name="g" + nm, align_bytes=64)
+            return grps[b, nm]
 
-        def stage1(b):
-            (cA, sA), (cL, sL), (cT, sT), (cV, sV) = state[("q", b)]
-            cg = comb.tile([P, 2, S, PACK], BF16, name="cg", align_bytes=64)
-            cc = comb.tile([P, 2, S], U32, name="cc", align_bytes=64)
-            cs = comb.tile([P, 2, S], U8, name="cs", align_bytes=64)
-            for g, (xc, xs, yc, ys) in enumerate(((cV, sV, cT, sT), (cL, sL, cA, sA))):
-                for k in range(NT):
-                    cp = ps_c.tile([P, PACK, P], F32, name="cp")
-                    cols = slice(P * k, P * k + P)
-                    for t in range(PACK):
-                        mcols = slice(P * t, P * t + P)
-                        nc.tensor.matmul_mx(
-                            out=cp[:, t, :],
-                            lhsT=xc[:, mcols].bitcast(FP8X4),
-                            lhsT_scale=xs[:, mcols],
-                            rhs=yc[:, cols].bitcast(FP8X4),
-                            rhs_scale=ys[:, cols],
-                            start=True,
-                            stop=True,
-                        )
-                    nc.scalar.copy(out=cg[:, g, cols, :], in_=cp[:].rearrange("p t s -> p s t"))
-                nc.vector.quantize_mx(
-                    out=cc[:, g, :].bitcast(FP8X4),
-                    scales=cs[:, g, :],
-                    in_=cg[:, g].rearrange("p s t -> p (s t)"),
-                )
-            state[("c", b)] = (cc, cs)
+        turned = {}
 
-        def stage2(b):
-            cc, cs = state[("c", b)]
-            w = epi.tile([P, NT, D], F32, name="w", bufs=2)
-            y = epi.tile([P, NT, D], F32, name="y")
-            sums = small.tile([P, NT], F32, name="sums")
-            negmean = small.tile([P, NT], F32, name="negmean")
-            ssq = small.tile([P, NT], F32, name="ssq")
-            std = small.tile([P, NT], F32, name="std")
-            rstd = small.tile([P, NT], F32, name="rstd")
-            for i in range(NT):
-                hp = ps_h.tile([P, D], F32, name="hp")
-                cols = slice(P * i, P * i + P)
-                for g in range(2):
-                    nc.tensor.matmul_mx(
-                        out=hp[:],
-                        lhsT=cc[:, g, cols].bitcast(FP8X4),
-                        lhsT_scale=cs[:, g, cols],
-                        rhs=Wc[:, g, :].bitcast(FP8X4),
-                        rhs_scale=Ws[:, g, :],
-                        start=(g == 0),
-                        stop=(g == 1),
+        def turn(b, h):
+            if not 0 <= b < B:
+                return
+            xt = ps_t.tile([P, 2, 2 * P], F32, name="xt")
+            for ii in range(2):
+                words = raws[b]["A"][:, 2 * h + ii, :].bitcast(F32)
+                for u in range(2):
+                    nc.tensor.transpose(
+                        xt[:, u, P * ii : P * ii + P], words[:, P * u : P * u + P], ident[:]
                     )
-                nc.vector.scalar_tensor_tensor(
-                    out=w[:, i, :], in0=hp[:], scalar=1.0, in1=ob_b[:],
-                    op0=ALU.mult, op1=ALU.add, accum_out=sums[:, i : i + 1],
-                )
-            nc.vector.tensor_scalar(
-                out=negmean[:], in0=sums[:], scalar1=-1.0 / D, scalar2=None, op0=ALU.mult
+            turned[b, h] = xt
+
+        def turn_out(b, h):
+            if not 0 <= b < B:
+                return
+            g = grouped(b, "T")
+            g32 = g[:].rearrange("p s t -> p (s t)").bitcast(F32).rearrange("p (s u) -> p s u", u=2)
+            nc.scalar.copy(
+                out=g32[:, 2 * P * h : 2 * P * h + 2 * P, :],
+                in_=turned[b, h][:].rearrange("p u s -> p s u"),
             )
-            for i in range(NT):
-                junk = epi.tile([P, D], BF16, name="junk")
-                nc.scalar.activation(
-                    out=junk[:], in_=w[:, i, :], func=ACT.Square,
-                    bias=negmean[:, i : i + 1], scale=1.0, accum_out=ssq[:, i : i + 1],
-                )
-            for i in range(NT):
-                nc.vector.scalar_tensor_tensor(
-                    out=y[:, i, :], in0=w[:, i, :], scalar=negmean[:, i : i + 1], in1=g_b[:],
-                    op0=ALU.add, op1=ALU.mult,
-                )
-            nc.scalar.activation(out=std[:], in_=ssq[:], func=ACT.Sqrt, bias=eps_t[:], scale=1.0 / D)
-            nc.vector.reciprocal(out=rstd[:], in_=std[:])
-            dst = out[b].rearrange("(i p) e -> p i e", p=P)
-            for i in range(NT):
-                nc.vector.scalar_tensor_tensor(
-                    out=y[:, i, :], in0=y[:, i, :], scalar=rstd[:, i : i + 1], in1=beta_b[:],
-                    op0=ALU.mult, op1=ALU.add,
-                )
+
+        def group(engine, b, nm, lo=0, hi=D):
+            if not 0 <= b < B:
+                return
+            dst, src = grouped(b, nm)[:, lo:hi, :], raws[b][nm][:, :, lo:hi]
+            if engine == "V":
+                regroup(nc.vector.tensor_copy, dst, src)
+            elif engine == "S":
+                regroup(nc.scalar.copy, dst, src)
+            else:
                 nc.gpsimd.tensor_scalar(
-                    out=y[:, i, :], in0=y[:, i, :], scalar1=BIG, scalar2=0.0, op0=ALU.min, op1=ALU.max
+                    out=dst, in0=src.rearrange("p t d -> p d t"),
+                    scalar1=1.0, scalar2=0.0, op0=ALU.mult, op1=ALU.add,
                 )
-                nc.sync.dma_start(out=dst[:, i, :], in_=y[:, i, :])
 
-        load(0)
-        for v, vec in enumerate((ob, og, obeta)):
-            nc.sync.dma_start(out=vecs[0:1, v, :], in_=vec.unsqueeze(0))
-        rawW = const.tile([P, 2 * PACK, D], BF16)
-        nc.sync.dma_start(out=rawW[:], in_=oW.rearrange("(j p) n -> p j n", p=P))
-        load(1)
-        prep(0)
+        def quant(b, nm):
+            if not 0 <= b < B:
+                return
+            cw = code.tile([P, S], U32, name="cw" + nm, align_bytes=64)
+            sc = code.tile([P, S], U8, name="sc" + nm, align_bytes=64)
+            nc.vector.quantize_mx(
+                out=cw[:].bitcast(FP8X4), scales=sc[:],
+                in_=grps[b, nm][:].rearrange("p w t -> p (w t)"),
+            )
+            codes[b, nm] = (cw, sc)
 
-        bp = ps_h.tile([P, D], F32, name="hp")
-        nc.tensor.matmul(out=bp[:], lhsT=ones[:], rhs=vecs[:, 0, :], start=True, stop=True)
+        def stage1(b, g, k):
+            if not 0 <= b < B:
+                return
+            if b not in combs:
+                combs[b] = (
+                    comb.tile([P, 2, S, PACK], BF16, name="cg", align_bytes=64),
+                    comb.tile([P, 2, S], U32, name="cc", align_bytes=64),
+                    comb.tile([P, 2, S], U8, name="cs", align_bytes=64),
+                    {},
+                )
+            (xc, xs), (yc, ys) = [codes[b, nm] for nm in (("V", "T"), ("L", "A"))[g]]
+            cp = ps_c.tile([P, PACK, P], F32, name="cp")
+            cols = slice(P * k, P * k + P)
+            for t in range(PACK):
+                mcols = slice(P * t, P * t + P)
+                nc.tensor.matmul_mx(
+                    out=cp[:, t, :],
+                    lhsT=xc[:, mcols].bitcast(FP8X4), lhsT_scale=xs[:, mcols],
+                    rhs=yc[:, cols].bitcast(FP8X4), rhs_scale=ys[:, cols],
+                    start=True, stop=True,
+                )
+            combs[b][3][g, k] = cp
+
+        def comb_out(b, g, k):
+            if not 0 <= b < B:
+                return
+            cg, cps = combs[b][0], combs[b][3]
+            nc.scalar.copy(
+                out=cg[:, g, P * k : P * k + P, :], in_=cps[g, k][:].rearrange("p t s -> p s t")
+            )
+
+        def quant_comb(b, g):
+            if not 0 <= b < B:
+                return
+            cg, cc, cs, cps = combs[b]
+            nc.vector.quantize_mx(
+                out=cc[:, g, :].bitcast(FP8X4), scales=cs[:, g, :],
+                in_=cg[:, g].rearrange("p s t -> p (s t)"),
+            )
+
+        def ln_tiles(b):
+            lns[b] = {
+                "w": epi.tile([P, NT, D], F32, name="w", bufs=2),
+                "y": epi.tile([P, NT, D], F32, name="y"),
+                "sums": small.tile([P, NT], F32, name="sums"),
+                "negmean": small.tile([P, NT], F32, name="negmean"),
+                "ssq": small.tile([P, NT], F32, name="ssq"),
+                "std": small.tile([P, NT], F32, name="std"),
+                "rstd": small.tile([P, NT], F32, name="rstd"),
+            }
+
+        def stage2(b, i):
+            if not 0 <= b < B:
+                return
+            if b not in lns:
+                ln_tiles(b)
+            cc, cs = combs[b][1], combs[b][2]
+            hp = ps_h.tile([P, D], F32, name="hp")
+            cols = slice(P * i, P * i + P)
+            for g in range(2):
+                nc.tensor.matmul_mx(
+                    out=hp[:],
+                    lhsT=cc[:, g, cols].bitcast(FP8X4), lhsT_scale=cs[:, g, cols],
+                    rhs=Wc[:, g, :].bitcast(FP8X4), rhs_scale=Ws[:, g, :],
+                    start=(g == 0), stop=(g == 1),
+                )
+            lns[b]["hp", i] = hp
+
+        def ln_sum(b, i):
+            t = lns[b]
+            nc.vector.scalar_tensor_tensor(
+                out=t["w"][:, i, :], in0=t["hp", i][:], scalar=1.0, in1=ob_b[:],
+                op0=ALU.mult, op1=ALU.add, accum_out=t["sums"][:, i : i + 1],
+            )
+
+        def ln_mean(b):
+            t = lns[b]
+            nc.vector.tensor_scalar(
+                out=t["negmean"][:], in0=t["sums"][:], scalar1=-1.0 / D, scalar2=None, op0=ALU.mult
+            )
+
+        def ln_square(b, i):
+            t = lns[b]
+            junk = epi.tile([P, D], BF16, name="junk")
+            nc.scalar.activation(
+                out=junk[:], in_=t["w"][:, i, :], func=ACT.Square,
+                bias=t["negmean"][:, i : i + 1], scale=1.0, accum_out=t["ssq"][:, i : i + 1],
+            )
+
+        def ln_gain(b, i):
+            t = lns[b]
+            nc.vector.scalar_tensor_tensor(
+                out=t["y"][:, i, :], in0=t["w"][:, i, :], scalar=t["negmean"][:, i : i + 1],
+                in1=g_b[:], op0=ALU.add, op1=ALU.mult,
+            )
+
+        def ln_std(b):
+            t = lns[b]
+            nc.scalar.activation(
+                out=t["std"][:], in_=t["ssq"][:], func=ACT.Sqrt, bias=eps_t[:], scale=1.0 / D
+            )
+
+        def ln_rstd(b):
+            t = lns[b]
+            nc.vector.reciprocal(out=t["rstd"][:], in_=t["std"][:])
+
+        def ln_shift(b, i):
+            t = lns[b]
+            nc.vector.scalar_tensor_tensor(
+                out=t["y"][:, i, :], in0=t["y"][:, i, :], scalar=t["rstd"][:, i : i + 1],
+                in1=beta_b[:], op0=ALU.mult, op1=ALU.add,
+            )
+
+        def relu_store(b, i):
+            y = lns[b]["y"]
+            nc.gpsimd.tensor_scalar(
+                out=y[:, i, :], in0=y[:, i, :], scalar1=BIG, scalar2=0.0, op0=ALU.min, op1=ALU.max
+            )
+            nc.sync.dma_start(out=out[b].rearrange("(i p) e -> p i e", p=P)[:, i, :], in_=y[:, i, :])
+
         ob_b = const.tile([P, D], F32)
-        nc.scalar.copy(out=ob_b[:], in_=bp[:])
         g_b = ps_k.tile([P, D], F32)
-        nc.tensor.matmul(out=g_b[:], lhsT=ones[:], rhs=vecs[:, 1, :], start=True, stop=True)
         beta_b = ps_k.tile([P, D], F32)
-        nc.tensor.matmul(out=beta_b[:], lhsT=ones[:], rhs=vecs[:, 2, :], start=True, stop=True)
-
+        rawW = const.tile([P, 2 * PACK, D], BF16)
         gW = const.tile([P, 2, D, PACK], BF16, align_bytes=64)
         Wc = const.tile([P, 2, D], U32, align_bytes=64)
         Ws = const.tile([P, 2, D], U8, align_bytes=64)
-        for g in range(2):
-            regroup(nc.scalar.copy, gW[:, g], rawW[:, PACK * g : PACK * g + PACK, :])
-        for g in range(2):
+
+        def vectors():
+            bp = ps_h.tile([P, D], F32, name="hp")
+            for v, dst in enumerate((bp, g_b, beta_b)):
+                nc.tensor.matmul(out=dst[:], lhsT=ones[:], rhs=vecs[:, v, :], start=True, stop=True)
+            nc.scalar.copy(out=ob_b[:], in_=bp[:])
+
+        def group_w(g):
+            regroup(nc.vector.tensor_copy, gW[:, g], rawW[:, PACK * g : PACK * g + PACK, :])
+
+        def quant_w(g):
             nc.vector.quantize_mx(
-                out=Wc[:, g, :].bitcast(FP8X4),
-                scales=Ws[:, g, :],
+                out=Wc[:, g, :].bitcast(FP8X4), scales=Ws[:, g, :],
                 in_=gW[:, g].rearrange("p n t -> p (n t)"),
             )
 
-        for b in range(B):
-            if b + 2 < B:
-                load(b + 2)
-            stage1(b)
-            if b + 1 < B:
-                prep(b + 1)
-            stage2(b)
+        ctx.enter_context(tc.manual_schedule())
+        load(0)
+        for v, vec in enumerate((ob, og, obeta)):
+            nc.sync.dma_start(out=vecs[0:1, v, :], in_=vec.unsqueeze(0))
+        nc.sync.dma_start(out=rawW[:], in_=oW.rearrange("(j p) n -> p j n", p=P))
+        load(1)
+        load(2)
+        load(3)
+
+        turn(0, 0)
+        turn_out(0, 0)
+        turn(0, 1)
+        turn_out(0, 1)
+        group("V", 0, "V")
+        group("V", 0, "A")
+        quant(0, "V")
+        quant(0, "T")
+        stage1(0, 0, 0)
+        stage1(0, 0, 1)
+        group("S", 0, "L")
+        quant(0, "A")
+        quant(0, "L")
+        vectors()
+        turn(1, 0)
+        for i in range(NT):
+            comb_out(0, 0, i)
+            stage1(0, *((0, 2), (0, 3), (1, 0), (1, 1))[i])
+        group_w(0)
+        group_w(1)
+        quant_w(0)
+        quant_comb(0, 0)
+        for i in range(NT):
+            comb_out(0, 1, i)
+            if i < 2:
+                stage1(0, 1, i + 2)
+        turn_out(1, 0)
+        turn(1, 1)
+        turn_out(1, 1)
+        turn(2, 0)
+        group("V", 1, "A")
+        quant_w(1)
+        quant_comb(0, 1)
+        stage2(0, 0)
+        stage2(0, 1)
+        stage2(0, 2)
+        group("V", 1, "V")
+        quant(1, "T")
+        quant(1, "V")
+        stage1(1, 0, 0)
+        stage1(1, 0, 1)
+        group("V", 1, "L")
+        quant(1, "L")
+        group("S", 2, "V")
+        turn_out(2, 0)
+        turn(2, 1)
+        turn_out(2, 1)
+        turn(3, 0)
+        group("S", 2, "L")
+
+        for n in range(B):
+            load(n + 4)
+            ln_sum(n, 0)
+            stage2(n, 3)
+            comb_out(n + 1, 0, 0)
+            stage1(n + 1, 0, 2)
+            ln_sum(n, 1)
+            comb_out(n + 1, 0, 1)
+            stage1(n + 1, 0, 3)
+            quant(n + 1, "A")
+            for i in range(NT):
+                group("G", n + 2, "A", P * i, P * i + P)
+            ln_sum(n, 2)
+            turn_out(n + 3, 0)
+            turn(n + 3, 1)
+            ln_sum(n, 3)
+            for i in range(2):
+                comb_out(n + 1, 0, i + 2)
+                stage1(n + 1, 1, i)
+            ln_mean(n)
+            for i in range(NT):
+                ln_gain(n, i)
+                ln_square(n, i)
+            ln_std(n)
+            quant_comb(n + 1, 0)
+            quant(n + 2, "T")
+            ln_rstd(n)
+            for i in range(NT):
+                ln_shift(n, i)
+                relu_store(n, i)
+                comb_out(n + 1, 1, i)
+                if i < 2:
+                    stage1(n + 1, 1, i + 2)
+                if i == 1:
+                    turn_out(n + 3, 1)
+                    turn(n + 4, 0)
+            quant_comb(n + 1, 1)
+            stage2(n + 1, 0)
+            stage2(n + 1, 1)
+            group("V", n + 3, "L", 0, LV)
+            quant(n + 2, "V")
+            stage1(n + 2, 0, 0)
+            stage1(n + 2, 0, 1)
+            stage2(n + 1, 2)
+            quant(n + 2, "L")
+            group("S", n + 3, "V")
+            group("S", n + 3, "L", LV, D)

@@ -18,7 +18,6 @@ P = 128
 PACK = 4
 NT = S // P
 EPS = 1e-5
-LV = 128
 BIG = 3.0e38
 
 FLOPS = 2 * B * S * S * D * 2 + 2 * B * S * (2 * D) * D
@@ -45,7 +44,7 @@ def tile_clawmatrix_pb_t_kernel(tc, A, vp, lp, oW, ob, og, obeta, out):
         ps_t = ctx.enter_context(tc.psum_pool(name="ps_t", bufs=1))
         ps_c = ctx.enter_context(tc.psum_pool(name="ps_c", bufs=2))
         ps_k = ctx.enter_context(tc.psum_pool(name="ps_k", bufs=1))
-        ps_h = ctx.enter_context(tc.psum_pool(name="ps_h", bufs=3))
+        ps_h = ctx.enter_context(tc.psum_pool(name="ps_h", bufs=4))
 
         eps_t = const.tile([P, 1], F32)
         nc.vector.memset(eps_t[:], EPS)
@@ -160,13 +159,14 @@ def tile_clawmatrix_pb_t_kernel(tc, A, vp, lp, oW, ob, og, obeta, out):
                 out=cg[:, g, P * k : P * k + P, :], in_=cps[g, k][:].rearrange("p t s -> p s t")
             )
 
-        def quant_comb(b, g):
+        def quant_comb(b):
             if not 0 <= b < B:
                 return
             cg, cc, cs, cps = combs[b]
             nc.vector.quantize_mx(
-                out=cc[:, g, :].bitcast(FP8X4), scales=cs[:, g, :],
-                in_=cg[:, g].rearrange("p s t -> p (s t)"),
+                out=cc[:].rearrange("p g s -> p (g s)").bitcast(FP8X4),
+                scales=cs[:].rearrange("p g s -> p (g s)"),
+                in_=cg[:].rearrange("p g s t -> p (g s t)"),
             )
 
         def ln_tiles(b):
@@ -250,7 +250,7 @@ def tile_clawmatrix_pb_t_kernel(tc, A, vp, lp, oW, ob, og, obeta, out):
             nc.sync.dma_start(out=out[b].rearrange("(i p) e -> p i e", p=P)[:, i, :], in_=y[:, i, :])
 
         ob_b = const.tile([P, D], F32)
-        g_b = ps_k.tile([P, D], F32)
+        g_b = const.tile([P, D], F32)
         beta_b = ps_k.tile([P, D], F32)
         rawW = const.tile([P, 2 * PACK, D], BF16)
         gW = const.tile([P, 2, D, PACK], BF16, align_bytes=64)
@@ -259,9 +259,11 @@ def tile_clawmatrix_pb_t_kernel(tc, A, vp, lp, oW, ob, og, obeta, out):
 
         def vectors():
             bp = ps_h.tile([P, D], F32, name="hp")
-            for v, dst in enumerate((bp, g_b, beta_b)):
+            gp = ps_h.tile([P, D], F32, name="hp")
+            for v, dst in enumerate((bp, gp, beta_b)):
                 nc.tensor.matmul(out=dst[:], lhsT=ones[:], rhs=vecs[:, v, :], start=True, stop=True)
             nc.scalar.copy(out=ob_b[:], in_=bp[:])
+            nc.scalar.copy(out=g_b[:], in_=gp[:])
 
         def group_w(g):
             regroup(nc.vector.tensor_copy, gW[:, g], rawW[:, PACK * g : PACK * g + PACK, :])
@@ -302,79 +304,89 @@ def tile_clawmatrix_pb_t_kernel(tc, A, vp, lp, oW, ob, og, obeta, out):
         group_w(0)
         group_w(1)
         quant_w(0)
-        quant_comb(0, 0)
-        for i in range(NT):
-            comb_out(0, 1, i)
-            if i < 2:
-                stage1(0, 1, i + 2)
+        quant_w(1)
         turn_out(1, 0)
         turn(1, 1)
+        comb_out(0, 1, 0)
+        stage1(0, 1, 2)
+        comb_out(0, 1, 1)
+        stage1(0, 1, 3)
         turn_out(1, 1)
         turn(2, 0)
-        group("V", 1, "A")
-        quant_w(1)
-        quant_comb(0, 1)
-        stage2(0, 0)
-        stage2(0, 1)
-        stage2(0, 2)
+        comb_out(0, 1, 2)
+        comb_out(0, 1, 3)
         group("V", 1, "V")
         quant(1, "T")
         quant(1, "V")
         stage1(1, 0, 0)
         stage1(1, 0, 1)
+        quant_comb(0)
+        for i in range(NT):
+            stage2(0, i)
+        group("V", 1, "A")
+        quant(1, "A")
         group("V", 1, "L")
         quant(1, "L")
-        group("S", 2, "V")
+        for i in range(3):
+            group("G", 2, "A", P * i, P * i + P)
         turn_out(2, 0)
         turn(2, 1)
+        group("S", 2, "V", 0, D // 2)
+        group("S", 2, "V", D // 2, D)
+        for i in range(NT):
+            comb_out(1, 0, i)
+            stage1(1, *((0, 2), (0, 3), (1, 0), (1, 1))[i])
         turn_out(2, 1)
         turn(3, 0)
-        group("S", 2, "L")
+        for i in range(NT):
+            comb_out(1, 1, i)
+            if i < 2:
+                stage1(1, 1, i + 2)
+                group("S", 2, "L", D // 2 * (i % 2), D // 2 * (i % 2) + D // 2)
 
         for n in range(B):
             load(n + 4)
-            ln_sum(n, 0)
-            stage2(n, 3)
-            comb_out(n + 1, 0, 0)
-            stage1(n + 1, 0, 2)
-            ln_sum(n, 1)
-            comb_out(n + 1, 0, 1)
-            stage1(n + 1, 0, 3)
-            quant(n + 1, "A")
             for i in range(NT):
-                group("G", n + 2, "A", P * i, P * i + P)
-            ln_sum(n, 2)
-            turn_out(n + 3, 0)
-            turn(n + 3, 1)
-            ln_sum(n, 3)
-            for i in range(2):
-                comb_out(n + 1, 0, i + 2)
-                stage1(n + 1, 1, i)
-            ln_mean(n)
-            for i in range(NT):
-                ln_gain(n, i)
-                ln_square(n, i)
-            ln_std(n)
-            quant_comb(n + 1, 0)
+                ln_sum(n, i)
             quant(n + 2, "T")
-            ln_rstd(n)
-            for i in range(NT):
-                ln_shift(n, i)
-                relu_store(n, i)
-                comb_out(n + 1, 1, i)
-                if i < 2:
-                    stage1(n + 1, 1, i + 2)
-                if i == 1:
-                    turn_out(n + 3, 1)
-                    turn(n + 4, 0)
-            quant_comb(n + 1, 1)
-            stage2(n + 1, 0)
-            stage2(n + 1, 1)
-            group("V", n + 3, "L", 0, LV)
+            ln_mean(n)
             quant(n + 2, "V")
             stage1(n + 2, 0, 0)
             stage1(n + 2, 0, 1)
-            stage2(n + 1, 2)
+            for i in range(NT):
+                ln_gain(n, i)
+                ln_square(n, i)
+                if i in (1, 2):
+                    comb_out(n + 2, 0, i - 1)
+                    stage1(n + 2, 0, i + 1)
+            ln_std(n)
             quant(n + 2, "L")
-            group("S", n + 3, "V")
-            group("S", n + 3, "L", LV, D)
+            group("V", n + 2, "A", 3 * P, D)
+            quant_comb(n + 1)
+            for i in range(NT):
+                stage2(n + 1, i)
+            ln_rstd(n)
+            quant(n + 2, "A")
+            turn_out(n + 3, 0)
+            turn(n + 3, 1)
+            comb_out(n + 2, 0, 2)
+            stage1(n + 2, 1, 0)
+            comb_out(n + 2, 0, 3)
+            stage1(n + 2, 1, 1)
+            group("S", n + 3, "V", 0, D // 2)
+            group("S", n + 3, "V", D // 2, D)
+            comb_out(n + 2, 1, 0)
+            stage1(n + 2, 1, 2)
+            turn_out(n + 3, 1)
+            comb_out(n + 2, 1, 1)
+            stage1(n + 2, 1, 3)
+            turn(n + 4, 0)
+            group("S", n + 3, "L", 0, D // 2)
+            comb_out(n + 2, 1, 2)
+            group("S", n + 3, "L", D // 2, D)
+            comb_out(n + 2, 1, 3)
+            for i in range(NT):
+                if i < 3:
+                    group("G", n + 3, "A", P * i, P * i + P)
+                ln_shift(n, i)
+                relu_store(n, i)

@@ -18,6 +18,7 @@ P = 128
 PACK = 4
 NT = S // P
 EPS = 1e-5
+LV = 128
 BIG = 3.0e38
 
 FLOPS = 2 * B * S * S * D * 2 + 2 * B * S * (2 * D) * D
@@ -362,6 +363,7 @@ def tile_clawmatrix_pb_t_kernel(tc, A, vp, lp, oW, ob, og, obeta, out):
             ln_std(n)
             quant(n + 2, "L")
             group("V", n + 2, "A", 3 * P, D)
+            group("V", n + 3, "L", 0, LV)
             quant_comb(n + 1)
             for i in range(NT):
                 stage2(n + 1, i)
@@ -381,9 +383,8 @@ def tile_clawmatrix_pb_t_kernel(tc, A, vp, lp, oW, ob, og, obeta, out):
             comb_out(n + 2, 1, 1)
             stage1(n + 2, 1, 3)
             turn(n + 4, 0)
-            group("S", n + 3, "L", 0, D // 2)
             comb_out(n + 2, 1, 2)
-            group("S", n + 3, "L", D // 2, D)
+            group("S", n + 3, "L", LV, D)
             comb_out(n + 2, 1, 3)
             for i in range(NT):
                 if i < 3:

@@ -18,7 +18,6 @@ P = 128
 PACK = 4
 NT = S // P
 EPS = 1e-5
-LV = 128
 BIG = 3.0e38
 
 FLOPS = 2 * B * S * S * D * 2 + 2 * B * S * (2 * D) * D
@@ -53,6 +52,8 @@ def tile_clawmatrix_pb_t_kernel(tc, A, vp, lp, oW, ob, og, obeta, out):
         nc.scalar.activation(out=warm[:], in_=eps_t[:], func=ACT.Sqrt)
         ident = const.tile([P, P], F32)
         make_identity(nc, ident[:])
+        ident_b = const.tile([P, P], BF16)
+        make_identity(nc, ident_b[:])
         ones = const.tile([P, P], BF16)
         nc.vector.memset(ones[:], 1.0)
         vecs = const.tile([P, 3, D], BF16)
@@ -118,6 +119,30 @@ def tile_clawmatrix_pb_t_kernel(tc, A, vp, lp, oW, ob, og, obeta, out):
                     scalar1=1.0, scalar2=0.0, op0=ALU.mult, op1=ALU.add,
                 )
 
+        sided = {}
+
+        def side(b, nm, h):
+            if not 0 <= b < B:
+                return
+            up = ps_h.tile([P, 2, P * PACK], BF16, name="hp")
+            for j in range(2):
+                d0 = 2 * P * h + P * j
+                nc.tensor.matmul(
+                    out=up[:, j, :].rearrange("p (d t) -> p t d", t=PACK),
+                    lhsT=ident_b[:], rhs=raws[b][nm][:, :, d0 : d0 + P],
+                    start=True, stop=True,
+                )
+            sided[b, nm, h] = up
+
+        def side_out(b, nm, h):
+            if not 0 <= b < B:
+                return
+            g32 = grouped(b, nm)[:].rearrange("p d t -> p (d t)").bitcast(F32)
+            nc.scalar.copy(
+                out=g32[:, 4 * P * h : 4 * P * h + 4 * P],
+                in_=sided[b, nm, h][:].rearrange("p j x -> p (j x)").bitcast(F32),
+            )
+
         def quant(b, nm):
             if not 0 <= b < B:
                 return
@@ -160,14 +185,13 @@ def tile_clawmatrix_pb_t_kernel(tc, A, vp, lp, oW, ob, og, obeta, out):
                 out=cg[:, g, P * k : P * k + P, :], in_=cps[g, k][:].rearrange("p t s -> p s t")
             )
 
-        def quant_comb(b):
+        def quant_comb(b, g):
             if not 0 <= b < B:
                 return
             cg, cc, cs, cps = combs[b]
             nc.vector.quantize_mx(
-                out=cc[:].rearrange("p g s -> p (g s)").bitcast(FP8X4),
-                scales=cs[:].rearrange("p g s -> p (g s)"),
-                in_=cg[:].rearrange("p g s t -> p (g s t)"),
+                out=cc[:, g, :].bitcast(FP8X4), scales=cs[:, g, :],
+                in_=cg[:, g].rearrange("p s t -> p (s t)"),
             )
 
         def ln_tiles(b):
@@ -321,7 +345,8 @@ def tile_clawmatrix_pb_t_kernel(tc, A, vp, lp, oW, ob, og, obeta, out):
         quant(1, "V")
         stage1(1, 0, 0)
         stage1(1, 0, 1)
-        quant_comb(0)
+        quant_comb(0, 0)
+        quant_comb(0, 1)
         for i in range(NT):
             stage2(0, i)
         group("V", 1, "A")
@@ -338,17 +363,19 @@ def tile_clawmatrix_pb_t_kernel(tc, A, vp, lp, oW, ob, og, obeta, out):
             comb_out(1, 0, i)
             stage1(1, *((0, 2), (0, 3), (1, 0), (1, 1))[i])
         turn_out(2, 1)
-        turn(3, 0)
-        for i in range(NT):
+        group("S", 2, "L")
+        for i in range(2):
             comb_out(1, 1, i)
-            if i < 2:
-                stage1(1, 1, i + 2)
-                group("S", 2, "L", D // 2 * (i % 2), D // 2 * (i % 2) + D // 2)
 
         for n in range(B):
             load(n + 4)
             for i in range(NT):
                 ln_sum(n, i)
+                if i < 2:
+                    side(n + 3, "V", i)
+            turn(n + 3, 0)
+            stage1(n + 1, 1, 2)
+            stage1(n + 1, 1, 3)
             quant(n + 2, "T")
             ln_mean(n)
             quant(n + 2, "V")
@@ -357,35 +384,36 @@ def tile_clawmatrix_pb_t_kernel(tc, A, vp, lp, oW, ob, og, obeta, out):
             for i in range(NT):
                 ln_gain(n, i)
                 ln_square(n, i)
-                if i in (1, 2):
-                    comb_out(n + 2, 0, i - 1)
-                    stage1(n + 2, 0, i + 1)
+                if i < 2:
+                    side_out(n + 3, "V", i)
+                elif i == 2:
+                    comb_out(n + 1, 1, 2)
             ln_std(n)
+            comb_out(n + 1, 1, 3)
+            comb_out(n + 2, 0, 0)
+            stage1(n + 2, 0, 2)
             quant(n + 2, "L")
             group("V", n + 2, "A", 3 * P, D)
-            group("V", n + 3, "L", 0, LV)
-            quant_comb(n + 1)
-            for i in range(NT):
-                stage2(n + 1, i)
+            quant_comb(n + 1, 0)
             ln_rstd(n)
             quant(n + 2, "A")
+            quant_comb(n + 1, 1)
+            comb_out(n + 2, 0, 1)
+            stage1(n + 2, 0, 3)
             turn_out(n + 3, 0)
+            stage2(n + 1, 0)
+            stage2(n + 1, 1)
             turn(n + 3, 1)
+            stage2(n + 1, 2)
+            stage2(n + 1, 3)
             comb_out(n + 2, 0, 2)
             stage1(n + 2, 1, 0)
+            group("S", n + 3, "L", 0, D)
             comb_out(n + 2, 0, 3)
             stage1(n + 2, 1, 1)
-            group("S", n + 3, "V", 0, D // 2)
-            group("S", n + 3, "V", D // 2, D)
-            comb_out(n + 2, 1, 0)
-            stage1(n + 2, 1, 2)
             turn_out(n + 3, 1)
+            comb_out(n + 2, 1, 0)
             comb_out(n + 2, 1, 1)
-            stage1(n + 2, 1, 3)
-            turn(n + 4, 0)
-            comb_out(n + 2, 1, 2)
-            group("S", n + 3, "L", LV, D)
-            comb_out(n + 2, 1, 3)
             for i in range(NT):
                 if i < 3:
                     group("G", n + 3, "A", P * i, P * i + P)

@@ -124,23 +124,29 @@ def tile_clawmatrix_pb_t_kernel(tc, A, vp, lp, oW, ob, og, obeta, out):
         def side(b, nm, h):
             if not 0 <= b < B:
                 return
+            side_pe((b, nm, h), raws[b][nm], h)
+
+        def side_pe(key, src, h):
             up = ps_h.tile([P, 2, P * PACK], BF16, name="hp")
             for j in range(2):
                 d0 = 2 * P * h + P * j
                 nc.tensor.matmul(
                     out=up[:, j, :].rearrange("p (d t) -> p t d", t=PACK),
-                    lhsT=ident_b[:], rhs=raws[b][nm][:, :, d0 : d0 + P],
+                    lhsT=ident_b[:], rhs=src[:, :, d0 : d0 + P],
                     start=True, stop=True,
                 )
-            sided[b, nm, h] = up
+            sided[key] = up
 
         def side_out(b, nm, h):
             if not 0 <= b < B:
                 return
-            g32 = grouped(b, nm)[:].rearrange("p d t -> p (d t)").bitcast(F32)
+            side_copy((b, nm, h), grouped(b, nm)[:], h)
+
+        def side_copy(key, dst, h):
+            g32 = dst.rearrange("p d t -> p (d t)").bitcast(F32)
             nc.scalar.copy(
                 out=g32[:, 4 * P * h : 4 * P * h + 4 * P],
-                in_=sided[b, nm, h][:].rearrange("p j x -> p (j x)").bitcast(F32),
+                in_=sided[key][:].rearrange("p j x -> p (j x)").bitcast(F32),
             )
 
         def quant(b, nm):
@@ -247,7 +253,7 @@ def tile_clawmatrix_pb_t_kernel(tc, A, vp, lp, oW, ob, og, obeta, out):
             t = lns[b]
             nc.vector.scalar_tensor_tensor(
                 out=t["y"][:, i, :], in0=t["w"][:, i, :], scalar=t["negmean"][:, i : i + 1],
-                in1=g_b[:], op0=ALU.add, op1=ALU.mult,
+                in1=gb[:, 0, :], op0=ALU.add, op1=ALU.mult,
             )
 
         def ln_std(b):
@@ -264,7 +270,7 @@ def tile_clawmatrix_pb_t_kernel(tc, A, vp, lp, oW, ob, og, obeta, out):
             t = lns[b]
             nc.vector.scalar_tensor_tensor(
                 out=t["y"][:, i, :], in0=t["y"][:, i, :], scalar=t["rstd"][:, i : i + 1],
-                in1=beta_b[:], op0=ALU.mult, op1=ALU.add,
+                in1=gb[:, 1, :], op0=ALU.mult, op1=ALU.add,
             )
 
         def relu_store(b, i):
@@ -275,8 +281,7 @@ def tile_clawmatrix_pb_t_kernel(tc, A, vp, lp, oW, ob, og, obeta, out):
             nc.sync.dma_start(out=out[b].rearrange("(i p) e -> p i e", p=P)[:, i, :], in_=y[:, i, :])
 
         ob_b = const.tile([P, D], F32)
-        g_b = const.tile([P, D], F32)
-        beta_b = ps_k.tile([P, D], F32)
+        gb = ps_k.tile([P, 2, D], BF16)
         rawW = const.tile([P, 2 * PACK, D], BF16)
         gW = const.tile([P, 2, D, PACK], BF16, align_bytes=64)
         Wc = const.tile([P, 2, D], U32, align_bytes=64)
@@ -284,14 +289,19 @@ def tile_clawmatrix_pb_t_kernel(tc, A, vp, lp, oW, ob, og, obeta, out):
 
         def vectors():
             bp = ps_h.tile([P, D], F32, name="hp")
-            gp = ps_h.tile([P, D], F32, name="hp")
-            for v, dst in enumerate((bp, gp, beta_b)):
-                nc.tensor.matmul(out=dst[:], lhsT=ones[:], rhs=vecs[:, v, :], start=True, stop=True)
+            for v, dst in enumerate((bp[:], gb[:, 0, :], gb[:, 1, :])):
+                nc.tensor.matmul(out=dst, lhsT=ones[:], rhs=vecs[:, v, :], start=True, stop=True)
             nc.scalar.copy(out=ob_b[:], in_=bp[:])
-            nc.scalar.copy(out=g_b[:], in_=gp[:])
 
         def group_w(g):
             regroup(nc.vector.tensor_copy, gW[:, g], rawW[:, PACK * g : PACK * g + PACK, :])
+
+        def side_w(u):
+            g = u // 2
+            side_pe(("W", u), rawW[:, PACK * g : PACK * g + PACK, :], u % 2)
+
+        def side_w_out(u):
+            side_copy(("W", u), gW[:, u // 2], u % 2)
 
         def quant_w(g):
             nc.vector.quantize_mx(
@@ -340,82 +350,82 @@ def tile_clawmatrix_pb_t_kernel(tc, A, vp, lp, oW, ob, og, obeta, out):
         turn(2, 0)
         comb_out(0, 1, 2)
         comb_out(0, 1, 3)
-        group("V", 1, "V")
-        quant(1, "T")
-        quant(1, "V")
-        stage1(1, 0, 0)
-        stage1(1, 0, 1)
+        group("V", 1, "A")
+        group("V", 1, "L")
+        quant(1, "A")
+        quant(1, "L")
+        stage1(1, 1, 0)
+        stage1(1, 1, 1)
         quant_comb(0, 0)
         quant_comb(0, 1)
         for i in range(NT):
             stage2(0, i)
-        group("V", 1, "A")
-        quant(1, "A")
-        group("V", 1, "L")
-        quant(1, "L")
-        for i in range(3):
+        group("V", 1, "V")
+        quant(1, "T")
+        quant(1, "V")
+        for i in range(NT):
             group("G", 2, "A", P * i, P * i + P)
         turn_out(2, 0)
         turn(2, 1)
-        group("S", 2, "V", 0, D // 2)
-        group("S", 2, "V", D // 2, D)
-        for i in range(NT):
-            comb_out(1, 0, i)
-            stage1(1, *((0, 2), (0, 3), (1, 0), (1, 1))[i])
-        turn_out(2, 1)
         group("S", 2, "L")
-        for i in range(2):
+        for i in range(NT):
             comb_out(1, 1, i)
+            stage1(1, *((1, 2), (1, 3), (0, 0), (0, 1))[i])
+        turn_out(2, 1)
+        for i in range(2):
+            group("S", 2, "V", D // 2 * i, D // 2 * i + D // 2)
+            comb_out(1, 0, i)
 
         for n in range(B):
             load(n + 4)
-            for i in range(NT):
-                ln_sum(n, i)
-                if i < 2:
-                    side(n + 3, "V", i)
+            ln_sum(n, 0)
+            ln_sum(n, 1)
             turn(n + 3, 0)
-            stage1(n + 1, 1, 2)
-            stage1(n + 1, 1, 3)
-            quant(n + 2, "T")
+            stage1(n + 1, 0, 2)
+            stage1(n + 1, 0, 3)
+            for i in range(2):
+                side(n + 3, "V", i)
+            ln_sum(n, 2)
+            ln_sum(n, 3)
+            quant(n + 2, "L")
             ln_mean(n)
-            quant(n + 2, "V")
-            stage1(n + 2, 0, 0)
-            stage1(n + 2, 0, 1)
+            quant(n + 2, "A")
+            stage1(n + 2, 1, 0)
+            stage1(n + 2, 1, 1)
+            for i in range(3):
+                group("G", n + 3, "A", P * i, P * i + P)
             for i in range(NT):
                 ln_gain(n, i)
                 ln_square(n, i)
                 if i < 2:
-                    side_out(n + 3, "V", i)
-                elif i == 2:
-                    comb_out(n + 1, 1, 2)
+                    comb_out(n + 1, 0, i + 2)
             ln_std(n)
-            comb_out(n + 1, 1, 3)
-            comb_out(n + 2, 0, 0)
-            stage1(n + 2, 0, 2)
-            quant(n + 2, "L")
-            group("V", n + 2, "A", 3 * P, D)
-            quant_comb(n + 1, 0)
-            ln_rstd(n)
-            quant(n + 2, "A")
+            quant(n + 2, "T")
             quant_comb(n + 1, 1)
-            comb_out(n + 2, 0, 1)
-            stage1(n + 2, 0, 3)
+            ln_rstd(n)
+            quant(n + 2, "V")
+            quant_comb(n + 1, 0)
+            for i in range(2):
+                side_out(n + 3, "V", i)
+            comb_out(n + 2, 1, 0)
+            stage1(n + 2, 1, 2)
             turn_out(n + 3, 0)
             stage2(n + 1, 0)
             stage2(n + 1, 1)
             turn(n + 3, 1)
+            comb_out(n + 2, 1, 1)
+            stage1(n + 2, 1, 3)
             stage2(n + 1, 2)
             stage2(n + 1, 3)
-            comb_out(n + 2, 0, 2)
-            stage1(n + 2, 1, 0)
-            group("S", n + 3, "L", 0, D)
-            comb_out(n + 2, 0, 3)
-            stage1(n + 2, 1, 1)
+            group("S", n + 3, "L")
+            for i in range(2):
+                comb_out(n + 2, 1, i + 2)
+                stage1(n + 2, 0, i)
             turn_out(n + 3, 1)
-            comb_out(n + 2, 1, 0)
-            comb_out(n + 2, 1, 1)
+            for i in range(2):
+                comb_out(n + 2, 0, i)
             for i in range(NT):
-                if i < 3:
-                    group("G", n + 3, "A", P * i, P * i + P)
                 ln_shift(n, i)
                 relu_store(n, i)
+                if i == 0:
+                    group("G", n + 3, "A", 3 * P, D)

@@ -42,9 +42,9 @@ def tile_clawmatrix_pb_t_kernel(tc, A, vp, lp, oW, ob, og, obeta, out):
         epi = ctx.enter_context(tc.tile_pool(name="epi", bufs=3))
         small = ctx.enter_context(tc.tile_pool(name="small", bufs=3))
         ps_t = ctx.enter_context(tc.psum_pool(name="ps_t", bufs=1))
-        ps_c = ctx.enter_context(tc.psum_pool(name="ps_c", bufs=2))
+        ps_c = ctx.enter_context(tc.psum_pool(name="ps_c", bufs=3))
         ps_k = ctx.enter_context(tc.psum_pool(name="ps_k", bufs=1))
-        ps_h = ctx.enter_context(tc.psum_pool(name="ps_h", bufs=4))
+        ps_h = ctx.enter_context(tc.psum_pool(name="ps_h", bufs=3))
 
         eps_t = const.tile([P, 1], F32)
         nc.vector.memset(eps_t[:], EPS)
@@ -235,10 +235,11 @@ def tile_clawmatrix_pb_t_kernel(tc, A, vp, lp, oW, ob, og, obeta, out):
                 op0=ALU.mult, op1=ALU.add, accum_out=t["sums"][:, i : i + 1],
             )
 
-        def ln_mean(b):
+        def ln_mean(b, lo=0, hi=NT):
             t = lns[b]
             nc.vector.tensor_scalar(
-                out=t["negmean"][:], in0=t["sums"][:], scalar1=-1.0 / D, scalar2=None, op0=ALU.mult
+                out=t["negmean"][:, lo:hi], in0=t["sums"][:, lo:hi],
+                scalar1=-1.0 / D, scalar2=None, op0=ALU.mult,
             )
 
         def ln_square(b, i):
@@ -256,15 +257,15 @@ def tile_clawmatrix_pb_t_kernel(tc, A, vp, lp, oW, ob, og, obeta, out):
                 in1=gb[:, 0, :], op0=ALU.add, op1=ALU.mult,
             )
 
-        def ln_std(b):
+        def ln_std(b, lo=0, hi=NT):
             t = lns[b]
             nc.scalar.activation(
-                out=t["std"][:], in_=t["ssq"][:], func=ACT.Sqrt, bias=eps_t[:], scale=1.0 / D
+                out=t["std"][:, lo:hi], in_=t["ssq"][:, lo:hi], func=ACT.Sqrt, bias=eps_t[:], scale=1.0 / D
             )
 
-        def ln_rstd(b):
+        def ln_rstd(b, lo=0, hi=NT):
             t = lns[b]
-            nc.vector.reciprocal(out=t["rstd"][:], in_=t["std"][:])
+            nc.vector.reciprocal(out=t["rstd"][:, lo:hi], in_=t["std"][:, lo:hi])
 
         def ln_shift(b, i):
             t = lns[b]
@@ -273,11 +274,15 @@ def tile_clawmatrix_pb_t_kernel(tc, A, vp, lp, oW, ob, og, obeta, out):
                 in1=gb[:, 1, :], op0=ALU.mult, op1=ALU.add,
             )
 
-        def relu_store(b, i):
+        def relu_store(b, i, on_scalar=False):
             y = lns[b]["y"]
-            nc.gpsimd.tensor_scalar(
-                out=y[:, i, :], in0=y[:, i, :], scalar1=BIG, scalar2=0.0, op0=ALU.min, op1=ALU.max
-            )
+            if on_scalar:
+                nc.scalar.activation(out=y[:, i, :], in_=y[:, i, :], func=ACT.Relu)
+            else:
+                nc.gpsimd.tensor_scalar(
+                    out=y[:, i, :], in0=y[:, i, :],
+                    scalar1=BIG, scalar2=0.0, op0=ALU.min, op1=ALU.max,
+                )
             nc.sync.dma_start(out=out[b].rearrange("(i p) e -> p i e", p=P)[:, i, :], in_=y[:, i, :])
 
         ob_b = const.tile([P, D], F32)
@@ -326,8 +331,8 @@ def tile_clawmatrix_pb_t_kernel(tc, A, vp, lp, oW, ob, og, obeta, out):
         group("V", 0, "A")
         quant(0, "V")
         quant(0, "T")
-        stage1(0, 0, 0)
-        stage1(0, 0, 1)
+        for i in range(3):
+            stage1(0, 0, i)
         group("S", 0, "L")
         quant(0, "A")
         quant(0, "L")
@@ -335,7 +340,7 @@ def tile_clawmatrix_pb_t_kernel(tc, A, vp, lp, oW, ob, og, obeta, out):
         turn(1, 0)
         for i in range(NT):
             comb_out(0, 0, i)
-            stage1(0, *((0, 2), (0, 3), (1, 0), (1, 1))[i])
+            stage1(0, *((0, 3), (1, 0), (1, 1), (1, 2))[i])
         group_w(0)
         group_w(1)
         quant_w(0)
@@ -343,9 +348,8 @@ def tile_clawmatrix_pb_t_kernel(tc, A, vp, lp, oW, ob, og, obeta, out):
         turn_out(1, 0)
         turn(1, 1)
         comb_out(0, 1, 0)
-        stage1(0, 1, 2)
-        comb_out(0, 1, 1)
         stage1(0, 1, 3)
+        comb_out(0, 1, 1)
         turn_out(1, 1)
         turn(2, 0)
         comb_out(0, 1, 2)
@@ -354,52 +358,55 @@ def tile_clawmatrix_pb_t_kernel(tc, A, vp, lp, oW, ob, og, obeta, out):
         group("V", 1, "L")
         quant(1, "A")
         quant(1, "L")
-        stage1(1, 1, 0)
-        stage1(1, 1, 1)
+        for i in range(3):
+            stage1(1, 1, i)
         quant_comb(0, 0)
         quant_comb(0, 1)
-        for i in range(NT):
-            stage2(0, i)
         group("V", 1, "V")
+        for i in range(3):
+            stage2(0, i)
+        turn_out(2, 0)
+        turn(2, 1)
+        group("S", 2, "L", 0, D // 2)
         quant(1, "T")
         quant(1, "V")
         for i in range(NT):
             group("G", 2, "A", P * i, P * i + P)
-        turn_out(2, 0)
-        turn(2, 1)
-        group("S", 2, "L")
         for i in range(NT):
             comb_out(1, 1, i)
-            stage1(1, *((1, 2), (1, 3), (0, 0), (0, 1))[i])
+            stage1(1, *((1, 3), (0, 0), (0, 1), (0, 2))[i])
+            if i == 1:
+                group("S", 2, "L", D // 2, D)
         turn_out(2, 1)
         for i in range(2):
             group("S", 2, "V", D // 2 * i, D // 2 * i + D // 2)
             comb_out(1, 0, i)
 
-        for n in range(B):
+        ln_sum(0, 0)
+        stage2(0, 3)
+        for n in range(B - 2):
             load(n + 4)
-            ln_sum(n, 0)
             ln_sum(n, 1)
             turn(n + 3, 0)
-            stage1(n + 1, 0, 2)
             stage1(n + 1, 0, 3)
-            for i in range(2):
-                side(n + 3, "V", i)
+            side(n + 3, "V", 0)
             ln_sum(n, 2)
+            side(n + 3, "V", 1)
             ln_sum(n, 3)
             quant(n + 2, "L")
             ln_mean(n)
             quant(n + 2, "A")
-            stage1(n + 2, 1, 0)
-            stage1(n + 2, 1, 1)
+            for i in range(3):
+                stage1(n + 2, 1, i)
             for i in range(3):
                 group("G", n + 3, "A", P * i, P * i + P)
             for i in range(NT):
                 ln_gain(n, i)
                 ln_square(n, i)
-                if i < 2:
-                    comb_out(n + 1, 0, i + 2)
+                if i == 1:
+                    comb_out(n + 1, 0, 2)
             ln_std(n)
+            comb_out(n + 1, 0, 3)
             quant(n + 2, "T")
             quant_comb(n + 1, 1)
             ln_rstd(n)
@@ -407,25 +414,56 @@ def tile_clawmatrix_pb_t_kernel(tc, A, vp, lp, oW, ob, og, obeta, out):
             quant_comb(n + 1, 0)
             for i in range(2):
                 side_out(n + 3, "V", i)
-            comb_out(n + 2, 1, 0)
-            stage1(n + 2, 1, 2)
-            turn_out(n + 3, 0)
-            stage2(n + 1, 0)
-            stage2(n + 1, 1)
-            turn(n + 3, 1)
-            comb_out(n + 2, 1, 1)
-            stage1(n + 2, 1, 3)
-            stage2(n + 1, 2)
-            stage2(n + 1, 3)
-            group("S", n + 3, "L")
-            for i in range(2):
-                comb_out(n + 2, 1, i + 2)
-                stage1(n + 2, 0, i)
-            turn_out(n + 3, 1)
-            for i in range(2):
-                comb_out(n + 2, 0, i)
+            for i in range(3):
+                stage2(n + 1, i)
             for i in range(NT):
                 ln_shift(n, i)
                 relu_store(n, i)
                 if i == 0:
                     group("G", n + 3, "A", 3 * P, D)
+            ln_sum(n + 1, 0)
+            comb_out(n + 2, 1, 0)
+            stage1(n + 2, 1, 3)
+            turn_out(n + 3, 0)
+            turn(n + 3, 1)
+            comb_out(n + 2, 1, 1)
+            stage1(n + 2, 0, 0)
+            stage2(n + 1, 3)
+            group("S", n + 3, "L")
+            comb_out(n + 2, 1, 2)
+            stage1(n + 2, 0, 1)
+            comb_out(n + 2, 1, 3)
+            stage1(n + 2, 0, 2)
+            turn_out(n + 3, 1)
+            for i in range(2):
+                comb_out(n + 2, 0, i)
+
+        for n in (B - 2, B - 1):
+            ln_sum(n, 1)
+            stage1(n + 1, 0, 3)
+            ln_sum(n, 2)
+            ln_mean(n, 0, 2)
+            ln_sum(n, 3)
+            ln_gain(n, 0)
+            ln_mean(n, 2, 4)
+            for lo in (0, 2):
+                ln_square(n, lo)
+                comb_out(n + 1, 0, 2 + lo // 2)
+                ln_square(n, lo + 1)
+                ln_std(n, lo, lo + 2)
+            ln_gain(n, 1)
+            ln_gain(n, 2)
+            quant_comb(n + 1, 1)
+            ln_rstd(n, 0, 2)
+            ln_gain(n, 3)
+            quant_comb(n + 1, 0)
+            for i in range(3):
+                stage2(n + 1, i)
+            for i in range(NT):
+                ln_shift(n, i)
+                relu_store(n, i, on_scalar=n == B - 1 and i % 2 == 1)
+                if i == 0:
+                    ln_rstd(n, 2, 4)
+            if n + 1 < B:
+                ln_sum(n + 1, 0)
+                stage2(n + 1, 3)

@@ -18,6 +18,7 @@ P = 128
 PACK = 4
 NT = S // P
 EPS = 1e-5
+GA = 160
 BIG = 3.0e38
 
 FLOPS = 2 * B * S * S * D * 2 + 2 * B * S * (2 * D) * D
@@ -61,19 +62,22 @@ def tile_clawmatrix_pb_t_kernel(tc, A, vp, lp, oW, ob, og, obeta, out):
 
         raws, grps, codes, combs, lns = {}, {}, {}, {}, {}
 
-        def load(b):
+        def load(b, order="ALV"):
             if not 0 <= b < B:
                 return
-            rawA = raw.tile([P, NT, S], BF16, name="rawA")
-            nc.sync.dma_start(out=rawA[:], in_=A[b].rearrange("(i p) t -> p i t", p=P))
-            rawV = raw.tile([P, PACK, D], BF16, name="rawV")
-            nc.sync.dma_start(
-                out=rawV[:].rearrange("p (u e) d -> p u (e d)", e=2),
-                in_=vp[b].rearrange("(u p e) d -> p u (e d)", u=2, e=2),
-            )
-            rawL = raw.tile([P, NT, D], BF16, name="rawL")
-            nc.sync.dma_start(out=rawL[:], in_=lp[b].rearrange("(i p) d -> p i d", p=P))
-            raws[b] = {"A": rawA, "V": rawV, "L": rawL}
+            for nm in order:
+                t = raw.tile([P, NT, S], BF16, name="raw" + nm)
+                raws[b, nm] = t
+                if nm == "V":
+                    nc.sync.dma_start(
+                        out=t[:].rearrange("p (u e) d -> p u (e d)", e=2),
+                        in_=vp[b].rearrange("(u p e) d -> p u (e d)", u=2, e=2),
+                    )
+                else:
+                    src = A if nm == "A" else lp
+                    nc.sync.dma_start(
+                        out=t[:], in_=src[b].rearrange("(i p) t -> p i t", p=P)
+                    )
 
         def grouped(b, nm):
             if (b, nm) not in grps:
@@ -86,9 +90,12 @@ def tile_clawmatrix_pb_t_kernel(tc, A, vp, lp, oW, ob, og, obeta, out):
         def turn(b, h):
             if not 0 <= b < B:
                 return
-            xt = ps_t.tile([P, 2, 2 * P], F32, name="xt")
+            if (b, h) == (0, 1):
+                xt = ps_h.tile([P, 2, 2 * P], F32, name="hp")
+            else:
+                xt = ps_t.tile([P, 2, 2 * P], F32, name="xt")
             for ii in range(2):
-                words = raws[b]["A"][:, 2 * h + ii, :].bitcast(F32)
+                words = raws[b, "A"][:, 2 * h + ii, :].bitcast(F32)
                 for u in range(2):
                     nc.tensor.transpose(
                         xt[:, u, P * ii : P * ii + P], words[:, P * u : P * u + P], ident[:]
@@ -108,7 +115,7 @@ def tile_clawmatrix_pb_t_kernel(tc, A, vp, lp, oW, ob, og, obeta, out):
         def group(engine, b, nm, lo=0, hi=D):
             if not 0 <= b < B:
                 return
-            dst, src = grouped(b, nm)[:, lo:hi, :], raws[b][nm][:, :, lo:hi]
+            dst, src = grouped(b, nm)[:, lo:hi, :], raws[b, nm][:, :, lo:hi]
             if engine == "V":
                 regroup(nc.vector.tensor_copy, dst, src)
             elif engine == "S":
@@ -124,7 +131,7 @@ def tile_clawmatrix_pb_t_kernel(tc, A, vp, lp, oW, ob, og, obeta, out):
         def side(b, nm, h):
             if not 0 <= b < B:
                 return
-            side_pe((b, nm, h), raws[b][nm], h)
+            side_pe((b, nm, h), raws[b, nm], h)
 
         def side_pe(key, src, h):
             up = ps_h.tile([P, 2, P * PACK], BF16, name="hp")
@@ -296,7 +303,10 @@ def tile_clawmatrix_pb_t_kernel(tc, A, vp, lp, oW, ob, og, obeta, out):
             bp = ps_h.tile([P, D], F32, name="hp")
             for v, dst in enumerate((bp[:], gb[:, 0, :], gb[:, 1, :])):
                 nc.tensor.matmul(out=dst, lhsT=ones[:], rhs=vecs[:, v, :], start=True, stop=True)
-            nc.scalar.copy(out=ob_b[:], in_=bp[:])
+            sided["bias"] = bp
+
+        def bias_out():
+            nc.scalar.copy(out=ob_b[:], in_=sided["bias"][:])
 
         def group_w(g):
             regroup(nc.vector.tensor_copy, gW[:, g], rawW[:, PACK * g : PACK * g + PACK, :])
@@ -315,33 +325,37 @@ def tile_clawmatrix_pb_t_kernel(tc, A, vp, lp, oW, ob, og, obeta, out):
             )
 
         ctx.enter_context(tc.manual_schedule())
-        load(0)
+        load(0, "VAL")
+        load(1, "A")
         for v, vec in enumerate((ob, og, obeta)):
             nc.sync.dma_start(out=vecs[0:1, v, :], in_=vec.unsqueeze(0))
         nc.sync.dma_start(out=rawW[:], in_=oW.rearrange("(j p) n -> p j n", p=P))
-        load(1)
+        load(1, "LV")
         load(2)
         load(3)
 
         turn(0, 0)
-        turn_out(0, 0)
         turn(0, 1)
+        turn_out(0, 0)
         turn_out(0, 1)
         group("V", 0, "V")
         group("V", 0, "A")
         quant(0, "V")
+        quant(0, "A")
         quant(0, "T")
         for i in range(3):
             stage1(0, 0, i)
         group("S", 0, "L")
-        quant(0, "A")
+        group("V", 1, "A")
         quant(0, "L")
+        group_w(0)
         vectors()
         turn(1, 0)
         for i in range(NT):
             comb_out(0, 0, i)
             stage1(0, *((0, 3), (1, 0), (1, 1), (1, 2))[i])
-        group_w(0)
+            if i == 2:
+                bias_out()
         group_w(1)
         quant_w(0)
         quant_w(1)
@@ -354,15 +368,14 @@ def tile_clawmatrix_pb_t_kernel(tc, A, vp, lp, oW, ob, og, obeta, out):
         turn(2, 0)
         comb_out(0, 1, 2)
         comb_out(0, 1, 3)
-        group("V", 1, "A")
         group("V", 1, "L")
-        quant(1, "A")
+        group("V", 1, "V")
         quant(1, "L")
+        quant(1, "A")
         for i in range(3):
             stage1(1, 1, i)
         quant_comb(0, 0)
         quant_comb(0, 1)
-        group("V", 1, "V")
         for i in range(3):
             stage2(0, i)
         turn_out(2, 0)
@@ -370,20 +383,22 @@ def tile_clawmatrix_pb_t_kernel(tc, A, vp, lp, oW, ob, og, obeta, out):
         group("S", 2, "L", 0, D // 2)
         quant(1, "T")
         quant(1, "V")
+        group("V", 2, "V", 0, D // 2)
+        ln_sum(0, 0)
         for i in range(NT):
             group("G", 2, "A", P * i, P * i + P)
         for i in range(NT):
             comb_out(1, 1, i)
+            if i == 1:
+                stage2(0, 3)
             stage1(1, *((1, 3), (0, 0), (0, 1), (0, 2))[i])
             if i == 1:
                 group("S", 2, "L", D // 2, D)
         turn_out(2, 1)
-        for i in range(2):
-            group("S", 2, "V", D // 2 * i, D // 2 * i + D // 2)
-            comb_out(1, 0, i)
+        comb_out(1, 0, 0)
+        group("S", 2, "V", D // 2, D)
+        comb_out(1, 0, 1)
 
-        ln_sum(0, 0)
-        stage2(0, 3)
         for n in range(B - 2):
             load(n + 4)
             ln_sum(n, 1)
@@ -398,8 +413,8 @@ def tile_clawmatrix_pb_t_kernel(tc, A, vp, lp, oW, ob, og, obeta, out):
             quant(n + 2, "A")
             for i in range(3):
                 stage1(n + 2, 1, i)
-            for i in range(3):
-                group("G", n + 3, "A", P * i, P * i + P)
+            for i in range(2):
+                group("G", n + 3, "A", GA * i, GA * i + GA)
             for i in range(NT):
                 ln_gain(n, i)
                 ln_square(n, i)
@@ -417,11 +432,12 @@ def tile_clawmatrix_pb_t_kernel(tc, A, vp, lp, oW, ob, og, obeta, out):
             for i in range(3):
                 stage2(n + 1, i)
             for i in range(NT):
+                if i == 3:
+                    ln_sum(n + 1, 0)
                 ln_shift(n, i)
                 relu_store(n, i)
                 if i == 0:
-                    group("G", n + 3, "A", 3 * P, D)
-            ln_sum(n + 1, 0)
+                    group("G", n + 3, "A", 2 * GA, D)
             comb_out(n + 2, 1, 0)
             stage1(n + 2, 1, 3)
             turn_out(n + 3, 0)
@@ -464,6 +480,6 @@ def tile_clawmatrix_pb_t_kernel(tc, A, vp, lp, oW, ob, og, obeta, out):
                 relu_store(n, i, on_scalar=n == B - 1 and i % 2 == 1)
                 if i == 0:
                     ln_rstd(n, 2, 4)
-            if n + 1 < B:
-                ln_sum(n + 1, 0)
-                stage2(n + 1, 3)
+                if i == 2 and n + 1 < B:
+                    ln_sum(n + 1, 0)
+                    stage2(n + 1, 3)

from contextlib import ExitStack

import concourse.mybir as mybir
from concourse.masks import make_identity

F32 = mybir.dt.float32
BF16 = mybir.dt.bfloat16
U32 = mybir.dt.uint32
U8 = mybir.dt.uint8
FP8X4 = mybir.dt.float8_e4m3fn_x4
ALU = mybir.AluOpType
ACT = mybir.ActivationFunctionType

B = 8
S = 512
D = 512
P = 128
PACK = 4
NT = S // P
EPS = 1e-5
GA = 160
BIG = 3.0e38

FLOPS = 2 * B * S * S * D * 2 + 2 * B * S * (2 * D) * D


def regroup(copy, dst, src):
    copy(
        out=dst.rearrange("p (c i) t -> p c t i", i=4),
        in_=src.rearrange("p t (c i) -> p c t i", i=4),
    )


def tile_clawmatrix_pb_t_kernel(tc, A, vp, lp, oW, ob, og, obeta, out):
    nc = tc.nc
    with ExitStack() as ctx:
        const = ctx.enter_context(tc.tile_pool(name="const", bufs=1))
        raw = ctx.enter_context(tc.tile_pool(name="raw", bufs=4))
        grp = ctx.enter_context(tc.tile_pool(name="grp", bufs=2))
        grp1 = ctx.enter_context(tc.tile_pool(name="grp1", bufs=1))
        code = ctx.enter_context(tc.tile_pool(name="code", bufs=2))
        comb = ctx.enter_context(tc.tile_pool(name="comb", bufs=2))
        epi = ctx.enter_context(tc.tile_pool(name="epi", bufs=3))
        small = ctx.enter_context(tc.tile_pool(name="small", bufs=3))
        ps_t = ctx.enter_context(tc.psum_pool(name="ps_t", bufs=1))
        ps_c = ctx.enter_context(tc.psum_pool(name="ps_c", bufs=3))
        ps_k = ctx.enter_context(tc.psum_pool(name="ps_k", bufs=1))
        ps_h = ctx.enter_context(tc.psum_pool(name="ps_h", bufs=3))

        eps_t = const.tile([P, 1], F32)
        nc.vector.memset(eps_t[:], EPS)
        warm = const.tile([P, 1], F32)
        nc.scalar.activation(out=warm[:], in_=eps_t[:], func=ACT.Sqrt)
        ident = const.tile([P, P], F32)
        make_identity(nc, ident[:])
        ident_b = const.tile([P, P], BF16)
        make_identity(nc, ident_b[:])
        ones = const.tile([P, P], BF16)
        nc.vector.memset(ones[:], 1.0)
        vecs = const.tile([P, 3, D], BF16)
        nc.vector.memset(vecs[:], 0.0)

        raws, grps, codes, combs, lns = {}, {}, {}, {}, {}

        def load(b, order="ALV"):
            if not 0 <= b < B:
                return
            for nm in order:
                t = raw.tile([P, NT, S], BF16, name="raw" + nm)
                raws[b, nm] = t
                if nm == "V":
                    nc.sync.dma_start(
                        out=t[:].rearrange("p (u e) d -> p u (e d)", e=2),
                        in_=vp[b].rearrange("(u p e) d -> p u (e d)", u=2, e=2),
                    )
                else:
                    src = A if nm == "A" else lp
                    nc.sync.dma_start(
                        out=t[:], in_=src[b].rearrange("(i p) t -> p i t", p=P)
                    )

        def grouped(b, nm):
            if (b, nm) not in grps:
                pool = grp1 if nm == "A" else grp
                grps[b, nm] = pool.tile([P, S, PACK], BF16, name="g" + nm, align_bytes=64)
            return grps[b, nm]

        turned = {}

        def turn(b, h):
            if not 0 <= b < B:
                return
            if (b, h) == (0, 1):
                xt = ps_h.tile([P, 2, 2 * P], F32, name="hp")
            else:
                xt = ps_t.tile([P, 2, 2 * P], F32, name="xt")
            for ii in range(2):
                words = raws[b, "A"][:, 2 * h + ii, :].bitcast(F32)
                for u in range(2):
                    nc.tensor.transpose(
                        xt[:, u, P * ii : P * ii + P], words[:, P * u : P * u + P], ident[:]
                    )
            turned[b, h] = xt

        def turn_out(b, h):
            if not 0 <= b < B:
                return
            g = grouped(b, "T")
            g32 = g[:].rearrange("p s t -> p (s t)").bitcast(F32).rearrange("p (s u) -> p s u", u=2)
            nc.scalar.copy(
                out=g32[:, 2 * P * h : 2 * P * h + 2 * P, :],
                in_=turned[b, h][:].rearrange("p u s -> p s u"),
            )

        def group(engine, b, nm, lo=0, hi=D):
            if not 0 <= b < B:
                return
            dst, src = grouped(b, nm)[:, lo:hi, :], raws[b, nm][:, :, lo:hi]
            if engine == "V":
                regroup(nc.vector.tensor_copy, dst, src)
            elif engine == "S":
                regroup(nc.scalar.copy, dst, src)
            else:
                nc.gpsimd.tensor_scalar(
                    out=dst, in0=src.rearrange("p t d -> p d t"),
                    scalar1=1.0, scalar2=0.0, op0=ALU.mult, op1=ALU.add,
                )

        sided = {}

        def side(b, nm, h):
            if not 0 <= b < B:
                return
            side_pe((b, nm, h), raws[b, nm], h)

        def side_pe(key, src, h):
            up = ps_h.tile([P, 2, P * PACK], BF16, name="hp")
            for j in range(2):
                d0 = 2 * P * h + P * j
                nc.tensor.matmul(
                    out=up[:, j, :].rearrange("p (d t) -> p t d", t=PACK),
                    lhsT=ident_b[:], rhs=src[:, :, d0 : d0 + P],
                    start=True, stop=True,
                )
            sided[key] = up

        def side_out(b, nm, h):
            if not 0 <= b < B:
                return
            side_copy((b, nm, h), grouped(b, nm)[:], h)

        def side_copy(key, dst, h):
            g32 = dst.rearrange("p d t -> p (d t)").bitcast(F32)
            nc.scalar.copy(
                out=g32[:, 4 * P * h : 4 * P * h + 4 * P],
                in_=sided[key][:].rearrange("p j x -> p (j x)").bitcast(F32),
            )

        def quant(b, nm):
            if not 0 <= b < B:
                return
            cw = code.tile([P, S], U32, name="cw" + nm, align_bytes=64)
            sc = code.tile([P, S], U8, name="sc" + nm, align_bytes=64)
            nc.vector.quantize_mx(
                out=cw[:].bitcast(FP8X4), scales=sc[:],
                in_=grps[b, nm][:].rearrange("p w t -> p (w t)"),
            )
            codes[b, nm] = (cw, sc)

        def stage1(b, g, k):
            if not 0 <= b < B:
                return
            if b not in combs:
                combs[b] = (
                    comb.tile([P, 2, S, PACK], BF16, name="cg", align_bytes=64),
                    comb.tile([P, 2, S], U32, name="cc", align_bytes=64),
                    comb.tile([P, 2, S], U8, name="cs", align_bytes=64),
                    {},
                )
            (xc, xs), (yc, ys) = [codes[b, nm] for nm in (("V", "T"), ("L", "A"))[g]]
            cp = ps_c.tile([P, PACK, P], F32, name="cp")
            cols = slice(P * k, P * k + P)
            for t in range(PACK):
                mcols = slice(P * t, P * t + P)
                nc.tensor.matmul_mx(
                    out=cp[:, t, :],
                    lhsT=xc[:, mcols].bitcast(FP8X4), lhsT_scale=xs[:, mcols],
                    rhs=yc[:, cols].bitcast(FP8X4), rhs_scale=ys[:, cols],
                    start=True, stop=True,
                )
            combs[b][3][g, k] = cp

        def comb_out(b, g, k):
            if not 0 <= b < B:
                return
            cg, cps = combs[b][0], combs[b][3]
            nc.scalar.copy(
                out=cg[:, g, P * k : P * k + P, :], in_=cps[g, k][:].rearrange("p t s -> p s t")
            )

        def quant_comb(b, g):
            if not 0 <= b < B:
                return
            cg, cc, cs, cps = combs[b]
            nc.vector.quantize_mx(
                out=cc[:, g, :].bitcast(FP8X4), scales=cs[:, g, :],
                in_=cg[:, g].rearrange("p s t -> p (s t)"),
            )

        def ln_tiles(b):
            lns[b] = {
                "w": epi.tile([P, NT, D], F32, name="w", bufs=2),
                "y": epi.tile([P, NT, D], F32, name="y"),
                "sums": small.tile([P, NT], F32, name="sums"),
                "negmean": small.tile([P, NT], F32, name="negmean"),
                "ssq": small.tile([P, NT], F32, name="ssq"),
                "std": small.tile([P, NT], F32, name="std"),
                "rstd": small.tile([P, NT], F32, name="rstd"),
            }

        def stage2(b, i):
            if not 0 <= b < B:
                return
            if b not in lns:
                ln_tiles(b)
            cc, cs = combs[b][1], combs[b][2]
            hp = ps_h.tile([P, D], F32, name="hp")
            cols = slice(P * i, P * i + P)
            for g in range(2):
                nc.tensor.matmul_mx(
                    out=hp[:],
                    lhsT=cc[:, g, cols].bitcast(FP8X4), lhsT_scale=cs[:, g, cols],
                    rhs=Wc[:, g, :].bitcast(FP8X4), rhs_scale=Ws[:, g, :],
                    start=(g == 0), stop=(g == 1),
                )
            lns[b]["hp", i] = hp

        def ln_sum(b, i):
            t = lns[b]
            nc.vector.scalar_tensor_tensor(
                out=t["w"][:, i, :], in0=t["hp", i][:], scalar=1.0, in1=ob_b[:],
                op0=ALU.mult, op1=ALU.add, accum_out=t["sums"][:, i : i + 1],
            )

        def ln_mean(b, lo=0, hi=NT):
            t = lns[b]
            nc.vector.tensor_scalar(
                out=t["negmean"][:, lo:hi], in0=t["sums"][:, lo:hi],
                scalar1=-1.0 / D, scalar2=None, op0=ALU.mult,
            )

        def ln_square(b, i):
            t = lns[b]
            junk = epi.tile([P, D], BF16, name="junk")
            nc.scalar.activation(
                out=junk[:], in_=t["w"][:, i, :], func=ACT.Square,
                bias=t["negmean"][:, i : i + 1], scale=1.0, accum_out=t["ssq"][:, i : i + 1],
            )

        def ln_gain(b, i):
            t = lns[b]
            nc.vector.scalar_tensor_tensor(
                out=t["y"][:, i, :], in0=t["w"][:, i, :], scalar=t["negmean"][:, i : i + 1],
                in1=gb[:, 0, :], op0=ALU.add, op1=ALU.mult,
            )

        def ln_std(b, lo=0, hi=NT):
            t = lns[b]
            nc.scalar.activation(
                out=t["std"][:, lo:hi], in_=t["ssq"][:, lo:hi], func=ACT.Sqrt, bias=eps_t[:], scale=1.0 / D
            )

        def ln_rstd(b, lo=0, hi=NT):
            t = lns[b]
            nc.vector.reciprocal(out=t["rstd"][:, lo:hi], in_=t["std"][:, lo:hi])

        def ln_shift(b, i):
            t = lns[b]
            nc.vector.scalar_tensor_tensor(
                out=t["y"][:, i, :], in0=t["y"][:, i, :], scalar=t["rstd"][:, i : i + 1],
                in1=gb[:, 1, :], op0=ALU.mult, op1=ALU.add,
            )

        def relu_store(b, i, on_scalar=False):
            y = lns[b]["y"]
            if on_scalar:
                nc.scalar.activation(out=y[:, i, :], in_=y[:, i, :], func=ACT.Relu)
            else:
                nc.gpsimd.tensor_scalar(
                    out=y[:, i, :], in0=y[:, i, :],
                    scalar1=BIG, scalar2=0.0, op0=ALU.min, op1=ALU.max,
                )
            nc.sync.dma_start(out=out[b].rearrange("(i p) e -> p i e", p=P)[:, i, :], in_=y[:, i, :])

        ob_b = const.tile([P, D], F32)
        gb = ps_k.tile([P, 2, D], BF16)
        rawW = const.tile([P, 2 * PACK, D], BF16)
        gW = const.tile([P, 2, D, PACK], BF16, align_bytes=64)
        Wc = const.tile([P, 2, D], U32, align_bytes=64)
        Ws = const.tile([P, 2, D], U8, align_bytes=64)

        def vectors():
            bp = ps_h.tile([P, D], F32, name="hp")
            for v, dst in enumerate((bp[:], gb[:, 0, :], gb[:, 1, :])):
                nc.tensor.matmul(out=dst, lhsT=ones[:], rhs=vecs[:, v, :], start=True, stop=True)
            sided["bias"] = bp

        def bias_out():
            nc.scalar.copy(out=ob_b[:], in_=sided["bias"][:])

        def group_w(g):
            regroup(nc.vector.tensor_copy, gW[:, g], rawW[:, PACK * g : PACK * g + PACK, :])

        def side_w(u):
            g = u // 2
            side_pe(("W", u), rawW[:, PACK * g : PACK * g + PACK, :], u % 2)

        def side_w_out(u):
            side_copy(("W", u), gW[:, u // 2], u % 2)

        def quant_w(g):
            nc.vector.quantize_mx(
                out=Wc[:, g, :].bitcast(FP8X4), scales=Ws[:, g, :],
                in_=gW[:, g].rearrange("p n t -> p (n t)"),
            )

        ctx.enter_context(tc.manual_schedule())
        load(0, "VAL")
        load(1, "A")
        for v, vec in enumerate((ob, og, obeta)):
            nc.sync.dma_start(out=vecs[0:1, v, :], in_=vec.unsqueeze(0))
        nc.sync.dma_start(out=rawW[:], in_=oW.rearrange("(j p) n -> p j n", p=P))
        load(1, "LV")
        load(2)
        load(3)

        turn(0, 0)
        turn(0, 1)
        turn_out(0, 0)
        turn_out(0, 1)
        group("V", 0, "V")
        group("V", 0, "A")
        quant(0, "V")
        quant(0, "A")
        quant(0, "T")
        for i in range(3):
            stage1(0, 0, i)
        group("S", 0, "L")
        group("V", 1, "A")
        quant(0, "L")
        group_w(0)
        vectors()
        turn(1, 0)
        for i in range(NT):
            comb_out(0, 0, i)
            stage1(0, *((0, 3), (1, 0), (1, 1), (1, 2))[i])
            if i == 2:
                bias_out()
        group_w(1)
        quant_w(0)
        quant_w(1)
        turn_out(1, 0)
        turn(1, 1)
        comb_out(0, 1, 0)
        stage1(0, 1, 3)
        comb_out(0, 1, 1)
        turn_out(1, 1)
        turn(2, 0)
        comb_out(0, 1, 2)
        comb_out(0, 1, 3)
        group("V", 1, "L")
        group("V", 1, "V")
        quant(1, "L")
        quant(1, "A")
        for i in range(3):
            stage1(1, 1, i)
        quant_comb(0, 0)
        quant_comb(0, 1)
        for i in range(3):
            stage2(0, i)
        turn_out(2, 0)
        turn(2, 1)
        group("S", 2, "L", 0, D // 2)
        quant(1, "T")
        quant(1, "V")
        group("V", 2, "V", 0, D // 2)
        ln_sum(0, 0)
        for i in range(NT):
            group("G", 2, "A", P * i, P * i + P)
        for i in range(NT):
            comb_out(1, 1, i)
            if i == 1:
                stage2(0, 3)
            stage1(1, *((1, 3), (0, 0), (0, 1), (0, 2))[i])
            if i == 1:
                group("S", 2, "L", D // 2, D)
        turn_out(2, 1)
        comb_out(1, 0, 0)
        group("S", 2, "V", D // 2, D)
        comb_out(1, 0, 1)

        for n in range(B - 2):
            load(n + 4)
            ln_sum(n, 1)
            turn(n + 3, 0)
            stage1(n + 1, 0, 3)
            side(n + 3, "V", 0)
            ln_sum(n, 2)
            side(n + 3, "V", 1)
            ln_sum(n, 3)
            quant(n + 2, "L")
            ln_mean(n)
            quant(n + 2, "A")
            for i in range(3):
                stage1(n + 2, 1, i)
            for i in range(2):
                group("G", n + 3, "A", GA * i, GA * i + GA)
            for i in range(NT):
                ln_gain(n, i)
                ln_square(n, i)
                if i == 1:
                    comb_out(n + 1, 0, 2)
            ln_std(n)
            comb_out(n + 1, 0, 3)
            quant(n + 2, "T")
            quant_comb(n + 1, 1)
            ln_rstd(n)
            quant(n + 2, "V")
            quant_comb(n + 1, 0)
            for i in range(2):
                side_out(n + 3, "V", i)
            for i in range(3):
                stage2(n + 1, i)
            for i in range(NT):
                if i == 3:
                    ln_sum(n + 1, 0)
                ln_shift(n, i)
                relu_store(n, i)
                if i == 0:
                    group("G", n + 3, "A", 2 * GA, D)
            comb_out(n + 2, 1, 0)
            stage1(n + 2, 1, 3)
            turn_out(n + 3, 0)
            turn(n + 3, 1)
            comb_out(n + 2, 1, 1)
            stage1(n + 2, 0, 0)
            stage2(n + 1, 3)
            group("S", n + 3, "L")
            comb_out(n + 2, 1, 2)
            stage1(n + 2, 0, 1)
            comb_out(n + 2, 1, 3)
            stage1(n + 2, 0, 2)
            turn_out(n + 3, 1)
            for i in range(2):
                comb_out(n + 2, 0, i)

        for n in (B - 2, B - 1):
            ln_sum(n, 1)
            stage1(n + 1, 0, 3)
            ln_sum(n, 2)
            ln_mean(n, 0, 2)
            ln_sum(n, 3)
            ln_gain(n, 0)
            ln_mean(n, 2, 4)
            for lo in (0, 2):
                ln_square(n, lo)
                comb_out(n + 1, 0, 2 + lo // 2)
                ln_square(n, lo + 1)
                ln_std(n, lo, lo + 2)
            ln_gain(n, 1)
            ln_gain(n, 2)
            quant_comb(n + 1, 1)
            ln_rstd(n, 0, 2)
            ln_gain(n, 3)
            quant_comb(n + 1, 0)
            for i in range(3):
                stage2(n + 1, i)
            for i in range(NT):
                ln_shift(n, i)
                relu_store(n, i, on_scalar=n == B - 1 and i % 2 == 1)
                if i == 0:
                    ln_rstd(n, 2, 4)
                if i == 2 and n + 1 < B:
                    ln_sum(n + 1, 0)
                    stage2(n + 1, 3)
